import numpy as np
import ml_dtypes


def mxq(x, axis, fmt="e4m3"):
    dtype, down = {"e4m3": (ml_dtypes.float8_e4m3fn, 7), "e5m2": (ml_dtypes.float8_e5m2, 14)}[fmt]
    v = np.moveaxis(np.asarray(x, np.float32).astype(ml_dtypes.bfloat16).astype(np.float64), axis, -1)
    blocks = v.reshape(v.shape[:-1] + (-1, 32))
    amax = np.abs(blocks).max(-1, keepdims=True)
    byte = np.maximum(np.where(amax > 0, np.frexp(amax)[1] - 1 + 127, 0) - down, 1)
    scale = np.exp2(byte - 127.0)
    codes = (blocks / scale).astype(np.float32).astype(dtype).astype(np.float64)
    return np.moveaxis((codes * scale).reshape(v.shape), -1, axis)


WIDE = False


def mx_kscale(k):
    if not WIDE:
        return np.ones(k)
    levels = np.array([10, -10, 5, -5, 0])
    a = np.random.permutation(np.resize(levels, k // 512 * 4)).reshape(k // 512, 4)
    idx = np.arange(k)
    return np.exp2(a[idx // 512, idx % 128 // 32])


BF16 = ml_dtypes.bfloat16


def bf(x):
    return np.asarray(x, np.float32).astype(BF16)


def f64(x):
    return np.asarray(x).astype(np.float64)


B, N, D, H, DH = 2, 4096, 512, 8, 64
INNER = H * DH
S = 2 * DH


def dpfp(u):
    u2 = np.concatenate([np.maximum(u, 0.0), np.maximum(-u, 0.0)], axis=-1)
    return u2 * np.roll(u2, 1, axis=-1)


def setup_inputs():
    s, t = mx_kscale(D), mx_kscale(N)
    f = dpfp(np.random.standard_normal((B, H, N, DH)))
    return {"x": bf(np.random.standard_normal((B, N, D)) * s),
            "wv": bf(np.random.standard_normal((D, INNER)) / np.sqrt(D) / s[:, None]),
            "beta": bf(np.random.standard_normal((B, H, N)) * t),
            "vo": bf(np.random.standard_normal((B, H, N, DH)) * 0.3),
            "k_phi": bf(f / f.sum(-1, keepdims=True) / t[:, None]),
            "W": bf(np.random.standard_normal((B, H, S, DH)))}


def reference(x, wv, beta, vo, k_phi, W):
    v = mxq(f64(x), 2, "e4m3") @ mxq(f64(wv), 0, "e4m3")
    v = v.reshape(B, N, H, DH).transpose(0, 2, 1, 3)
    dv = f64(beta)[..., None] * (v - f64(vo))
    return f64(W) + (mxq(f64(k_phi).transpose(0, 1, 3, 2), 3, "e4m3") @ mxq(dv, 2, "e4m3"))

@@ -1,0 +1,264 @@
+from contextlib import ExitStack
+
+import concourse.bass as bass
+import concourse.mybir as mybir
+import concourse.tile as tile
+from concourse.masks import make_identity
+
+FP8X4 = mybir.dt.float8_e4m3fn_x4
+BF16 = mybir.dt.bfloat16
+F32 = mybir.dt.float32
+U32 = mybir.dt.uint32
+U8 = mybir.dt.uint8
+ALU = mybir.AluOpType
+
+B, N, D, H, DH, S = 2, 4096, 512, 8, 64, 128
+P = 128
+FLOPS = 2 * B * N * D * (H * DH) + 2 * B * H * N * S * DH
+
+D0, NC, IL, R = 32, 4, 4, 8
+
+
+PIN = True
+G_SHARE = False
+T_LATE = [7, 9, 11, 13, 15, 17, 19, 20]
+
+
+def tile_dpfpattention_pb_t_kernel(tc, x, wv, beta, vo, k_phi, W, out):
+    nc = tc.nc
+    with ExitStack() as ctx:
+        const = ctx.enter_context(tc.tile_pool(name="const", bufs=1))
+        xraw_pool = ctx.enter_context(tc.tile_pool(name="xraw", bufs=3))
+        xg_pool = ctx.enter_context(tc.tile_pool(name="xg", bufs=3))
+        vo_pool = ctx.enter_context(tc.tile_pool(name="vo", bufs=4))
+        kraw_pool = ctx.enter_context(tc.tile_pool(name="kraw", bufs=4))
+        kg_pool = ctx.enter_context(tc.tile_pool(name="kg", bufs=3))
+        kw_pool = ctx.enter_context(tc.tile_pool(name="kw", bufs=4))
+        t_pool = ctx.enter_context(tc.tile_pool(name="t", bufs=4))
+        dv_pool = ctx.enter_context(tc.tile_pool(name="dv", bufs=3))
+        res_pool = ctx.enter_context(tc.tile_pool(name="res", bufs=2))
+        ps_acc = ctx.enter_context(tc.psum_pool(name="ps_acc", bufs=1))
+        ps_s1 = ctx.enter_context(tc.psum_pool(name="ps_s1", bufs=2))
+        ps_xt = ctx.enter_context(tc.psum_pool(name="ps_xt", bufs=2))
+        if PIN:
+            ctx.enter_context(tc.manual_schedule())
+
+        xv = x.rearrange("b (d0 c il r) k -> b c il d0 (r k)", d0=D0, c=NC, il=IL, r=R)
+        vv = vo.rearrange("b h (d0 c il r) d -> b c il d0 h (r d)", d0=D0, c=NC, il=IL, r=R)
+        kv = k_phi.rearrange("b h (d0 c il r) s -> b c il d0 h (r s)", d0=D0, c=NC, il=IL, r=R)
+        bv = beta.rearrange("b h (d0 c x) -> c (b h) d0 x", d0=D0, c=NC, x=IL * R)
+
+        xw = const.tile([P, 16, 512], U32, align_bytes=64)
+        xs = const.tile([P, 16, 512], U8, align_bytes=64)
+
+        xraws, voraws, kraws = {}, {}, {}
+        xts, xgs, kgs, kws, s1s, ts, dvgs, dvws = {}, {}, {}, {}, {}, {}, {}, {}
+        acc = [None] * 4
+
+        def where(s):
+            blk, rhi = divmod(s, 2)
+            return blk // 8, (blk // 4) % 2, blk % 4, rhi
+
+        def load_x(i):
+            b, c = divmod(i, NC)
+            xraw = xraw_pool.tile([P, R, D], BF16, name="xraw")
+            for il in range(IL):
+                nc.sync.dma_start(out=xraw[il:P:IL, :, :].rearrange("p r k -> p (r k)"), in_=xv[b, c, il])
+            xraws[i] = xraw
+
+        def load_blk(blk):
+            b, hf, c = blk // 8, (blk // 4) % 2, blk % 4
+            voraw = vo_pool.tile([P, 4, R, DH], BF16, name="voraw")
+            for il in range(IL):
+                nc.sync.dma_start(out=voraw[il:P:IL].rearrange("p h r d -> p h (r d)"), in_=vv[b, c, il][:, 4 * hf:4 * hf + 4, :])
+            kraw = kraw_pool.tile([P, 4, R, S], BF16, name="kraw")
+            for il in range(IL):
+                nc.sync.dma_start(out=kraw[il:P:IL].rearrange("p h r s -> p h (r s)"), in_=kv[b, c, il][:, 4 * hf:4 * hf + 4, :])
+            voraws[blk], kraws[blk] = voraw, kraw
+
+        def do_T(u):
+            x32 = xraws[u // 2][:].bitcast(F32)
+            rhi = u % 2
+            banks = []
+            for jp in range(2):
+                xt = ps_xt.tile([P, 2, 2, P], F32, name="xt", tag="xt")
+                for jl in range(2):
+                    for w in range(2):
+                        nc.tensor.transpose(xt[:, jl, w, :], x32[:, 4 * rhi + 2 * jp + jl, P * w:P * w + P], ident_f[:])
+                banks.append(xt)
+            xts[u] = banks
+
+        def do_X(u):
+            xg = xg_pool.tile([P, 4, P, 4], BF16, name="xg", align_bytes=64)
+            xg32 = xg[:].bitcast(F32)
+            for jp in range(2):
+                nc.scalar.copy(out=xg32[:, 2 * jp:2 * jp + 2, :, :], in_=xts[u][jp][:].rearrange("p jl w m -> p jl m w"))
+            xgs[u] = xg
+
+        def do_QX(u):
+            nc.vector.quantize_mx(out=xw[:, u, :].bitcast(FP8X4), scales=xs[:, u, :],
+                                  in_=xgs[u][:].rearrange("p j m t -> p (j m t)"))
+
+        def do_R(s):
+            rhi = s % 2
+            kg = kg_pool.tile([P, 4, S, 4], BF16, name="kg", align_bytes=64)
+            for hl in range(4):
+                nc.scalar.copy(out=kg[:, hl].rearrange("p (c i) t -> p c t i", i=4),
+                               in_=kraws[s // 2][:, hl, 4 * rhi:4 * rhi + 4, :].rearrange("p t (c i) -> p c t i", i=4))
+            kgs[s] = kg
+
+        def do_QK(s):
+            kw = kw_pool.tile([P, 512], U32, name="kw", align_bytes=64)
+            ks = kw_pool.tile([P, 512], U8, name="ks", align_bytes=64)
+            nc.vector.quantize_mx(out=kw[:].bitcast(FP8X4), scales=ks[:], in_=kgs[s][:].rearrange("p h s j -> p (h s j)"))
+            kws[s] = (kw, ks)
+
+        def do_S1(s):
+            b, hf, c, rhi = where(s)
+            unit = 8 * b + 2 * c + rhi
+            banks = []
+            for pr in range(2):
+                cg = 2 * hf + pr
+                s1 = ps_s1.tile([P, 4, P], F32, name="s1", tag="s1")
+                for j in range(4):
+                    nc.tensor.matmul_mx(out=s1[:, j, :],
+                                        lhsT=xw[:, unit, P * j:P * j + P].bitcast(FP8X4), lhsT_scale=xs[:, unit, P * j:P * j + P],
+                                        rhs=wvw[:, P * cg:P * cg + P].bitcast(FP8X4), rhs_scale=wvs[:, P * cg:P * cg + P],
+                                        start=True, stop=True)
+                banks.append(s1)
+            s1s[s] = banks
+
+        def do_A(s):
+            rhi = s % 2
+            t = t_pool.tile([P, 4, DH, 4], F32, name="t")
+            for pr in range(2):
+                nc.vector.tensor_tensor(out=t[:, 2 * pr:2 * pr + 2],
+                                        in0=s1s[s][pr][:].rearrange("p j (hh d) -> p hh d j", hh=2),
+                                        in1=voraws[s // 2][:, 2 * pr:2 * pr + 2, 4 * rhi:4 * rhi + 4, :].rearrange("p hh j d -> p hh d j"),
+                                        op=ALU.subtract)
+            ts[s] = t
+
+        def do_B(s, pr):
+            b, hf, c, rhi = where(s)
+            dvg = dv_pool.tile([P, 2, DH, 4], BF16, name="dvg%d" % pr, align_bytes=64, bufs=(1 if (pr == 1 and G_SHARE) else 3))
+            row0 = 16 * c + 8 * b + 4 * hf + 2 * pr
+            bb = beta_sb[:, 4 * rhi:4 * rhi + 4, row0:row0 + 2].rearrange("p j h -> p h j").unsqueeze(2).to_broadcast([P, 2, DH, 4])
+            eng = nc.gpsimd if (pr == 1 and G_SHARE and s < 31) else nc.vector
+            eng.tensor_tensor(out=dvg[:], in0=ts[s][:, 2 * pr:2 * pr + 2], in1=bb, op=ALU.mult)
+            dvgs[(s, pr)] = dvg
+
+        def do_QD(s, pr):
+            dvw = dv_pool.tile([P, P], U32, name="dvw%d" % pr, align_bytes=64)
+            dvs = dv_pool.tile([P, P], U8, name="dvs%d" % pr, align_bytes=64)
+            nc.vector.quantize_mx(out=dvw[:].bitcast(FP8X4), scales=dvs[:], in_=dvgs[(s, pr)][:].rearrange("p h d j -> p (h d j)"))
+            dvws[(s, pr)] = (dvw, dvs)
+
+        def do_S2(s, pr):
+            kw, ks = kws[s]
+            dvw, dvs = dvws[(s, pr)]
+            for hl in (2 * pr, 2 * pr + 1):
+                if s % 8 == 0:
+                    acc[hl] = ps_acc.tile([P, P], F32, name="acc%d" % hl, tag="acc%d" % hl)
+                nc.tensor.matmul_mx(out=acc[hl][:],
+                                    lhsT=kw[:, P * hl:P * hl + P].bitcast(FP8X4), lhsT_scale=ks[:, P * hl:P * hl + P],
+                                    rhs=dvw[:].bitcast(FP8X4), rhs_scale=dvs[:],
+                                    start=(s % 8 == 0), stop=(s % 8 == 7))
+
+        def do_FIN(ph, pr):
+            b, hf = divmod(ph, 2)
+            h0 = 4 * hf + 2 * pr
+            res = res_pool.tile([P, 2, DH], F32, name="res")
+            for e in range(2):
+                nc.vector.tensor_tensor(out=res[:, e, :], in0=acc[2 * pr + e][:, DH * e:DH * e + DH],
+                                        in1=w_sb[:, 8 * b + h0 + e, :], op=ALU.add)
+            nc.sync.dma_start(out=out[b, h0:h0 + 2].rearrange("h s d -> s h d"), in_=res[:])
+
+        load_x(0)
+        wraw = const.tile([P, 4, 512], BF16)
+        for w in range(2):
+            nc.sync.dma_start(out=wraw[:, 2 * w:2 * w + 2, :], in_=wv[256 * w:256 * w + 256, :].rearrange("(q e) c -> q e c", e=2))
+        bc = const.tile([P, 1024], BF16)
+        nc.vector.memset(bc[64:P, :], 0.0)
+        for c in range(NC):
+            nc.scalar.dma_start(out=bc[16 * c:16 * c + 16, :].rearrange("p (d0 x) -> p d0 x", x=IL * R), in_=bv[c])
+        w_sb = const.tile([P, 16, DH], BF16)
+        nc.scalar.dma_start(out=w_sb[:], in_=W.rearrange("b h s d -> s (b h) d"))
+        ident_f = const.tile([P, P], F32)
+        make_identity(nc, ident_f[:])
+        ident_b = const.tile([P, P], BF16)
+        make_identity(nc, ident_b[:])
+        load_blk(0)
+        load_x(1)
+        load_blk(1)
+        load_x(2)
+        load_blk(2)
+        load_blk(3)
+
+        bt = ps_s1.tile([P, R, P], BF16, name="bt", tag="s1")
+        bcv = bc[:].rearrange("p (q r) -> p q r", r=R)
+        for r in range(R):
+            nc.tensor.transpose(bt[:, r, :], bcv[:, :, r], ident_b[:])
+        beta_sb = const.tile([P, R, 64], F32)
+        nc.vector.tensor_copy(out=beta_sb[:], in_=bt[:, :, 0:64])
+        wgrp = const.tile([P, 512, 4], BF16, align_bytes=64)
+        wvw = const.tile([P, 512], U32, align_bytes=64)
+        wvs = const.tile([P, 512], U8, align_bytes=64)
+        nc.vector.tensor_copy(out=wgrp[:], in_=wraw[:].rearrange("p t c -> p c t"))
+        nc.vector.quantize_mx(out=wvw[:].bitcast(FP8X4), scales=wvs[:], in_=wgrp[:].rearrange("p c t -> p (c t)"))
+
+        t_step = {}
+        for u in range(16):
+            t_step[u] = u - 3 if u < 8 else T_LATE[u - 8]
+        x_emit = {}
+        for i in range(3, 8):
+            x_emit[i] = t_step[2 * i] - 5
+
+        lag = 1 if G_SHARE else 0
+        for s in range(-3, 33):
+            for u in range(16):
+                if t_step[u] == s - 1:
+                    do_X(u)
+            if 0 <= s < 32:
+                do_A(s)
+            for ph in range(4):
+                if s == 8 * (ph + 1):
+                    do_FIN(ph, 0)
+                if s == 8 * (ph + 1) + (lag if ph < 3 else 0):
+                    do_FIN(ph, 1)
+            if 0 <= s + 1 < 32:
+                do_S1(s + 1)
+            for u in range(16):
+                if t_step[u] == s:
+                    do_T(u)
+            if 0 <= s < 32:
+                do_B(s, 0)
+                if lag == 0:
+                    do_B(s, 1)
+            if 0 <= s + 2 < 32:
+                do_R(s + 2)
+            if 0 <= s + 1 < 32:
+                do_QK(s + 1)
+            for u in range(16):
+                if t_step[u] == s - 1:
+                    do_QX(u)
+            if 0 <= s < 32:
+                do_QD(s, 0)
+                do_S2(s, 0)
+            if lag == 0:
+                if 0 <= s < 32:
+                    do_QD(s, 1)
+                    do_S2(s, 1)
+            else:
+                if 0 <= s - 1 < 31:
+                    do_QD(s - 1, 1)
+                    do_S2(s - 1, 1)
+                if 0 <= s < 32:
+                    do_B(s, 1)
+                if s == 31:
+                    do_QD(s, 1)
+                    do_S2(s, 1)
+            for i in range(3, 8):
+                if x_emit[i] == s:
+                    load_x(i)
+            if (s + 7) % 2 == 0 and 4 <= (s + 7) // 2 < 16:
+                load_blk((s + 7) // 2)

@@ -20,7 +20,7 @@ D0, NC, IL, R = 32, 4, 4, 8
 
 
 PIN = True
-G_SHARE = False
+G_SHARE = True
 T_LATE = [7, 9, 11, 13, 15, 17, 19, 20]
 
 

@@ -19,9 +19,7 @@ FLOPS = 2 * B * N * D * (H * DH) + 2 * B * H * N * S * DH
 D0, NC, IL, R = 32, 4, 4, 8
 
 
-PIN = True
 G_SHARE = True
-T_LATE = [7, 9, 11, 13, 15, 17, 19, 20]
 
 
 def tile_dpfpattention_pb_t_kernel(tc, x, wv, beta, vo, k_phi, W, out):
@@ -29,52 +27,59 @@ def tile_dpfpattention_pb_t_kernel(tc, x, wv, beta, vo, k_phi, W, out):
     with ExitStack() as ctx:
         const = ctx.enter_context(tc.tile_pool(name="const", bufs=1))
         xraw_pool = ctx.enter_context(tc.tile_pool(name="xraw", bufs=3))
-        xg_pool = ctx.enter_context(tc.tile_pool(name="xg", bufs=3))
-        vo_pool = ctx.enter_context(tc.tile_pool(name="vo", bufs=4))
-        kraw_pool = ctx.enter_context(tc.tile_pool(name="kraw", bufs=4))
-        kg_pool = ctx.enter_context(tc.tile_pool(name="kg", bufs=3))
-        kw_pool = ctx.enter_context(tc.tile_pool(name="kw", bufs=4))
-        t_pool = ctx.enter_context(tc.tile_pool(name="t", bufs=4))
-        dv_pool = ctx.enter_context(tc.tile_pool(name="dv", bufs=3))
+        xg_pool = ctx.enter_context(tc.tile_pool(name="xg", bufs=2))
+        vo_pool = ctx.enter_context(tc.tile_pool(name="vo", bufs=3))
+        kraw_pool = ctx.enter_context(tc.tile_pool(name="kraw", bufs=3))
+        xw_pool = ctx.enter_context(tc.tile_pool(name="xw", bufs=8))
+        kg_pool = ctx.enter_context(tc.tile_pool(name="kg", bufs=2))
+        kw_pool = ctx.enter_context(tc.tile_pool(name="kw", bufs=2))
+        t_pool = ctx.enter_context(tc.tile_pool(name="t", bufs=3))
+        dv_pool = ctx.enter_context(tc.tile_pool(name="dv", bufs=2))
         res_pool = ctx.enter_context(tc.tile_pool(name="res", bufs=2))
-        ps_acc = ctx.enter_context(tc.psum_pool(name="ps_acc", bufs=1))
-        ps_s1 = ctx.enter_context(tc.psum_pool(name="ps_s1", bufs=2))
+        ps_acc = ctx.enter_context(tc.psum_pool(name="ps_acc", bufs=2))
+        ps_s1 = ctx.enter_context(tc.psum_pool(name="ps_s1", bufs=4))
         ps_xt = ctx.enter_context(tc.psum_pool(name="ps_xt", bufs=2))
-        if PIN:
-            ctx.enter_context(tc.manual_schedule())
+        ctx.enter_context(tc.manual_schedule())
 
-        xv = x.rearrange("b (d0 c il r) k -> b c il d0 (r k)", d0=D0, c=NC, il=IL, r=R)
+        xv = x.rearrange("b (d0 c il r) k -> b c il d0 r k", d0=D0, c=NC, il=IL, r=R)
         vv = vo.rearrange("b h (d0 c il r) d -> b c il d0 h (r d)", d0=D0, c=NC, il=IL, r=R)
         kv = k_phi.rearrange("b h (d0 c il r) s -> b c il d0 h (r s)", d0=D0, c=NC, il=IL, r=R)
         bv = beta.rearrange("b h (d0 c x) -> c (b h) d0 x", d0=D0, c=NC, x=IL * R)
 
-        xw = const.tile([P, 16, 512], U32, align_bytes=64)
-        xs = const.tile([P, 16, 512], U8, align_bytes=64)
+        part = const.tile([P, 16, DH], F32)
 
-        xraws, voraws, kraws = {}, {}, {}
-        xts, xgs, kgs, kws, s1s, ts, dvgs, dvws = {}, {}, {}, {}, {}, {}, {}, {}
-        acc = [None] * 4
+        xraws, voraws, kraws, xws = {}, {}, {}, {}
+        xts, xgs, kgs, kws, s1s, ts, dvgs, dvws, accs = {}, {}, {}, {}, {}, {}, {}, {}, {}
 
-        def where(s):
-            blk, rhi = divmod(s, 2)
-            return blk // 8, (blk // 4) % 2, blk % 4, rhi
+        def where(g):
+            return g // 8, (g // 4) % 2, g % 4
 
-        def load_x(i):
+        def load_x(i, pieces):
             b, c = divmod(i, NC)
             xraw = xraw_pool.tile([P, R, D], BF16, name="xraw")
-            for il in range(IL):
-                nc.sync.dma_start(out=xraw[il:P:IL, :, :].rearrange("p r k -> p (r k)"), in_=xv[b, c, il])
+            n = R // pieces
+            for q in range(pieces):
+                for il in range(IL):
+                    nc.sync.dma_start(out=xraw[il:P:IL, n * q:n * q + n, :], in_=xv[b, c, il][:, n * q:n * q + n, :])
             xraws[i] = xraw
 
-        def load_blk(blk):
-            b, hf, c = blk // 8, (blk // 4) % 2, blk % 4
-            voraw = vo_pool.tile([P, 4, R, DH], BF16, name="voraw")
-            for il in range(IL):
-                nc.sync.dma_start(out=voraw[il:P:IL].rearrange("p h r d -> p h (r d)"), in_=vv[b, c, il][:, 4 * hf:4 * hf + 4, :])
-            kraw = kraw_pool.tile([P, 4, R, S], BF16, name="kraw")
-            for il in range(IL):
-                nc.sync.dma_start(out=kraw[il:P:IL].rearrange("p h r s -> p h (r s)"), in_=kv[b, c, il][:, 4 * hf:4 * hf + 4, :])
-            voraws[blk], kraws[blk] = voraw, kraw
+        def load_vo(k, cls):
+            b, ch, hf = k // 4, (k // 2) % 2, k % 2
+            if k not in voraws:
+                voraws[k] = vo_pool.tile([P, 2, 4, R, DH], BF16, name="voraw")
+            for cl in cls:
+                for il in range(IL):
+                    nc.sync.dma_start(out=voraws[k][il:P:IL, cl].rearrange("p h r d -> p h (r d)"),
+                                      in_=vv[b, 2 * ch + cl, il][:, 4 * hf:4 * hf + 4, :])
+
+        def load_k(k):
+            b, ch, hf = k // 4, (k // 2) % 2, k % 2
+            kraw = kraw_pool.tile([P, 2, 4, R, S], BF16, name="kraw")
+            for cl in range(2):
+                for il in range(IL):
+                    nc.sync.dma_start(out=kraw[il:P:IL, cl].rearrange("p h r s -> p h (r s)"),
+                                      in_=kv[b, 2 * ch + cl, il][:, 4 * hf:4 * hf + 4, :])
+            kraws[k] = kraw
 
         def do_T(u):
             x32 = xraws[u // 2][:].bitcast(F32)
@@ -96,84 +101,89 @@ def tile_dpfpattention_pb_t_kernel(tc, x, wv, beta, vo, k_phi, W, out):
             xgs[u] = xg
 
         def do_QX(u):
-            nc.vector.quantize_mx(out=xw[:, u, :].bitcast(FP8X4), scales=xs[:, u, :],
-                                  in_=xgs[u][:].rearrange("p j m t -> p (j m t)"))
+            xw = xw_pool.tile([P, 512], U32, name="xw", align_bytes=64)
+            xs = xw_pool.tile([P, 512], U8, name="xs", align_bytes=64)
+            nc.vector.quantize_mx(out=xw[:].bitcast(FP8X4), scales=xs[:], in_=xgs[u][:].rearrange("p j m t -> p (j m t)"))
+            xws[u] = (xw, xs)
 
-        def do_R(s):
-            rhi = s % 2
-            kg = kg_pool.tile([P, 4, S, 4], BF16, name="kg", align_bytes=64)
-            for hl in range(4):
-                nc.scalar.copy(out=kg[:, hl].rearrange("p (c i) t -> p c t i", i=4),
-                               in_=kraws[s // 2][:, hl, 4 * rhi:4 * rhi + 4, :].rearrange("p t (c i) -> p c t i", i=4))
-            kgs[s] = kg
-
-        def do_QK(s):
-            kw = kw_pool.tile([P, 512], U32, name="kw", align_bytes=64)
-            ks = kw_pool.tile([P, 512], U8, name="ks", align_bytes=64)
-            nc.vector.quantize_mx(out=kw[:].bitcast(FP8X4), scales=ks[:], in_=kgs[s][:].rearrange("p h s j -> p (h s j)"))
-            kws[s] = (kw, ks)
-
-        def do_S1(s):
-            b, hf, c, rhi = where(s)
-            unit = 8 * b + 2 * c + rhi
-            banks = []
-            for pr in range(2):
-                cg = 2 * hf + pr
-                s1 = ps_s1.tile([P, 4, P], F32, name="s1", tag="s1")
-                for j in range(4):
-                    nc.tensor.matmul_mx(out=s1[:, j, :],
-                                        lhsT=xw[:, unit, P * j:P * j + P].bitcast(FP8X4), lhsT_scale=xs[:, unit, P * j:P * j + P],
-                                        rhs=wvw[:, P * cg:P * cg + P].bitcast(FP8X4), rhs_scale=wvs[:, P * cg:P * cg + P],
-                                        start=True, stop=True)
-                banks.append(s1)
-            s1s[s] = banks
-
-        def do_A(s):
-            rhi = s % 2
-            t = t_pool.tile([P, 4, DH, 4], F32, name="t")
-            for pr in range(2):
-                nc.vector.tensor_tensor(out=t[:, 2 * pr:2 * pr + 2],
-                                        in0=s1s[s][pr][:].rearrange("p j (hh d) -> p hh d j", hh=2),
-                                        in1=voraws[s // 2][:, 2 * pr:2 * pr + 2, 4 * rhi:4 * rhi + 4, :].rearrange("p hh j d -> p hh d j"),
-                                        op=ALU.subtract)
-            ts[s] = t
-
-        def do_B(s, pr):
-            b, hf, c, rhi = where(s)
-            dvg = dv_pool.tile([P, 2, DH, 4], BF16, name="dvg%d" % pr, align_bytes=64, bufs=(1 if (pr == 1 and G_SHARE) else 3))
-            row0 = 16 * c + 8 * b + 4 * hf + 2 * pr
-            bb = beta_sb[:, 4 * rhi:4 * rhi + 4, row0:row0 + 2].rearrange("p j h -> p h j").unsqueeze(2).to_broadcast([P, 2, DH, 4])
-            eng = nc.gpsimd if (pr == 1 and G_SHARE and s < 31) else nc.vector
-            eng.tensor_tensor(out=dvg[:], in0=ts[s][:, 2 * pr:2 * pr + 2], in1=bb, op=ALU.mult)
-            dvgs[(s, pr)] = dvg
-
-        def do_QD(s, pr):
-            dvw = dv_pool.tile([P, P], U32, name="dvw%d" % pr, align_bytes=64)
-            dvs = dv_pool.tile([P, P], U8, name="dvs%d" % pr, align_bytes=64)
-            nc.vector.quantize_mx(out=dvw[:].bitcast(FP8X4), scales=dvs[:], in_=dvgs[(s, pr)][:].rearrange("p h d j -> p (h d j)"))
-            dvws[(s, pr)] = (dvw, dvs)
-
-        def do_S2(s, pr):
-            kw, ks = kws[s]
-            dvw, dvs = dvws[(s, pr)]
-            for hl in (2 * pr, 2 * pr + 1):
-                if s % 8 == 0:
-                    acc[hl] = ps_acc.tile([P, P], F32, name="acc%d" % hl, tag="acc%d" % hl)
-                nc.tensor.matmul_mx(out=acc[hl][:],
-                                    lhsT=kw[:, P * hl:P * hl + P].bitcast(FP8X4), lhsT_scale=ks[:, P * hl:P * hl + P],
-                                    rhs=dvw[:].bitcast(FP8X4), rhs_scale=dvs[:],
-                                    start=(s % 8 == 0), stop=(s % 8 == 7))
-
-        def do_FIN(ph, pr):
-            b, hf = divmod(ph, 2)
-            h0 = 4 * hf + 2 * pr
-            res = res_pool.tile([P, 2, DH], F32, name="res")
+        def do_R(g):
+            pq = g % 4
+            kraw = kraws[g // 2]
+            kg = kg_pool.tile([P, 2, 4, S, 4], BF16, name="kg", align_bytes=64)
             for e in range(2):
-                nc.vector.tensor_tensor(out=res[:, e, :], in0=acc[2 * pr + e][:, DH * e:DH * e + DH],
-                                        in1=w_sb[:, 8 * b + h0 + e, :], op=ALU.add)
-            nc.sync.dma_start(out=out[b, h0:h0 + 2].rearrange("h s d -> s h d"), in_=res[:])
+                for ps in range(4):
+                    cl, rhi = divmod(ps, 2)
+                    nc.scalar.copy(out=kg[:, e, ps].rearrange("p (c i) t -> p c t i", i=4),
+                                   in_=kraw[:, cl, 2 * (pq % 2) + e, 4 * rhi:4 * rhi + 4, :].rearrange("p t (c i) -> p c t i", i=4))
+            kgs[g] = kg
 
-        load_x(0)
+        def do_QK(g):
+            kw = kw_pool.tile([P, 1024], U32, name="kw", align_bytes=64)
+            ks = kw_pool.tile([P, 1024], U8, name="ks", align_bytes=64)
+            nc.vector.quantize_mx(out=kw[:].bitcast(FP8X4), scales=ks[:], in_=kgs[g][:].rearrange("p e q s j -> p (e q s j)"))
+            kws[g] = (kw, ks)
+
+        def do_S1(g, ps):
+            pq = g % 4
+            xw, xs = xws[4 * (g // 4) + ps]
+            s1 = ps_s1.tile([P, 4, P], F32, name="s1", tag="s1")
+            for j in range(4):
+                nc.tensor.matmul_mx(out=s1[:, j, :],
+                                    lhsT=xw[:, P * j:P * j + P].bitcast(FP8X4), lhsT_scale=xs[:, P * j:P * j + P],
+                                    rhs=wvw[:, P * pq:P * pq + P].bitcast(FP8X4), rhs_scale=wvs[:, P * pq:P * pq + P],
+                                    start=True, stop=True)
+            s1s[(g, ps)] = s1
+
+        def do_A(g, ps):
+            pq = g % 4
+            cl, rhi = divmod(ps, 2)
+            if ps == 0:
+                ts[g] = t_pool.tile([P, 8, DH, 4], F32, name="t")
+            h0 = 2 * (pq % 2)
+            nc.vector.tensor_tensor(out=ts[g][:, 2 * ps:2 * ps + 2],
+                                    in0=s1s[(g, ps)][:].rearrange("p j (hh d) -> p hh d j", hh=2),
+                                    in1=voraws[g // 2][:, cl, h0:h0 + 2, 4 * rhi:4 * rhi + 4, :].rearrange("p hh j d -> p hh d j"),
+                                    op=ALU.subtract)
+
+        def do_B(g, half, eng):
+            dvg = dv_pool.tile([P, 4, DH, 4], BF16, name="dvg%d" % half, align_bytes=64, bufs=(1 if half == 1 else 2))
+            bb = beta2[:, g, 4 * half:4 * half + 4, :].unsqueeze(2).to_broadcast([P, 4, DH, 4])
+            eng.tensor_tensor(out=dvg[:], in0=ts[g][:, 4 * half:4 * half + 4], in1=bb, op=ALU.mult)
+            dvgs[(g, half)] = dvg
+
+        def do_QD(g, half):
+            dvw = dv_pool.tile([P, 256], U32, name="dvw%d" % half, align_bytes=64)
+            dvs = dv_pool.tile([P, 256], U8, name="dvs%d" % half, align_bytes=64)
+            nc.vector.quantize_mx(out=dvw[:].bitcast(FP8X4), scales=dvs[:], in_=dvgs[(g, half)][:].rearrange("p q d j -> p (q d j)"))
+            dvws[(g, half)] = (dvw, dvs)
+
+        def do_S2(g):
+            kw, ks = kws[g]
+            acc = ps_acc.tile([P, 4, DH], F32, name="acc", tag="acc")
+            av = acc[:].rearrange("p (e q) d -> p e (q d)", e=2)
+            for e in range(2):
+                for ps in range(4):
+                    dvw, dvs = dvws[(g, ps // 2)]
+                    o = (4 * e + ps) * P
+                    r0 = P * (ps % 2)
+                    nc.tensor.matmul_mx(out=av[:, e, :],
+                                        lhsT=kw[:, o:o + P].bitcast(FP8X4), lhsT_scale=ks[:, o:o + P],
+                                        rhs=dvw[:, r0:r0 + P].bitcast(FP8X4), rhs_scale=dvs[:, r0:r0 + P],
+                                        start=(ps == 0), stop=(ps == 3))
+            accs[g] = acc
+
+        def do_FIN(g):
+            b, ch, pq = where(g)
+            h0 = 8 * b + 2 * pq
+            valid = accs[g][:, 0:4:3, :]
+            if ch == 0:
+                nc.vector.tensor_tensor(out=part[:, h0:h0 + 2, :], in0=valid, in1=w_sb[:, h0:h0 + 2, :], op=ALU.add)
+            else:
+                res = res_pool.tile([P, 2, DH], F32, name="res")
+                nc.vector.tensor_tensor(out=res[:], in0=valid, in1=part[:, h0:h0 + 2, :], op=ALU.add)
+                nc.sync.dma_start(out=out[b, 2 * pq:2 * pq + 2].rearrange("h s d -> s h d"), in_=res[:])
+
+        load_x(0, 2)
         wraw = const.tile([P, 4, 512], BF16)
         for w in range(2):
             nc.sync.dma_start(out=wraw[:, 2 * w:2 * w + 2, :], in_=wv[256 * w:256 * w + 256, :].rearrange("(q e) c -> q e c", e=2))
@@ -183,82 +193,93 @@ def tile_dpfpattention_pb_t_kernel(tc, x, wv, beta, vo, k_phi, W, out):
             nc.scalar.dma_start(out=bc[16 * c:16 * c + 16, :].rearrange("p (d0 x) -> p d0 x", x=IL * R), in_=bv[c])
         w_sb = const.tile([P, 16, DH], BF16)
         nc.scalar.dma_start(out=w_sb[:], in_=W.rearrange("b h s d -> s (b h) d"))
-        ident_f = const.tile([P, P], F32)
-        make_identity(nc, ident_f[:])
         ident_b = const.tile([P, P], BF16)
         make_identity(nc, ident_b[:])
-        load_blk(0)
-        load_x(1)
-        load_blk(1)
-        load_x(2)
-        load_blk(2)
-        load_blk(3)
+        ident_f = const.tile([P, P], F32)
+        make_identity(nc, ident_f[:])
+        load_vo(0, [0])
+        load_x(1, 1)
+        load_vo(0, [1])
+        load_k(0)
+        load_x(2, 1)
+        load_vo(1, [0, 1])
+        load_k(1)
+        load_vo(2, [0, 1])
+        load_k(2)
 
         bt = ps_s1.tile([P, R, P], BF16, name="bt", tag="s1")
         bcv = bc[:].rearrange("p (q r) -> p q r", r=R)
         for r in range(R):
             nc.tensor.transpose(bt[:, r, :], bcv[:, :, r], ident_b[:])
-        beta_sb = const.tile([P, R, 64], F32)
-        nc.vector.tensor_copy(out=beta_sb[:], in_=bt[:, :, 0:64])
+        beta2 = const.tile([P, 16, 8, 4], F32)
+        for b in range(B):
+            for c in range(NC):
+                ch, cl = divmod(c, 2)
+                for rhi in range(2):
+                    g0 = 8 * b + 4 * ch
+                    q0 = 2 * (2 * cl + rhi)
+                    row0 = 16 * c + 8 * b
+                    nc.scalar.copy(out=beta2[:, g0:g0 + 4, q0:q0 + 2, :],
+                                   in_=bt[:, 4 * rhi:4 * rhi + 4, row0:row0 + 8].rearrange("p j (pq hh) -> p pq hh j", hh=2))
         wgrp = const.tile([P, 512, 4], BF16, align_bytes=64)
         wvw = const.tile([P, 512], U32, align_bytes=64)
         wvs = const.tile([P, 512], U8, align_bytes=64)
         nc.vector.tensor_copy(out=wgrp[:], in_=wraw[:].rearrange("p t c -> p c t"))
         nc.vector.quantize_mx(out=wvw[:].bitcast(FP8X4), scales=wvs[:], in_=wgrp[:].rearrange("p c t -> p (c t)"))
 
-        t_step = {}
-        for u in range(16):
-            t_step[u] = u - 3 if u < 8 else T_LATE[u - 8]
-        x_emit = {}
-        for i in range(3, 8):
-            x_emit[i] = t_step[2 * i] - 5
+        for u in range(4):
+            do_T(u)
+            do_X(u)
+            do_QX(u)
+            do_S1(0, u)
+            if u > 0:
+                do_A(0, u - 1)
+            if u == 1:
+                load_x(3, 1)
+        do_T(4)
 
-        lag = 1 if G_SHARE else 0
-        for s in range(-3, 33):
-            for u in range(16):
-                if t_step[u] == s - 1:
-                    do_X(u)
-            if 0 <= s < 32:
-                do_A(s)
-            for ph in range(4):
-                if s == 8 * (ph + 1):
-                    do_FIN(ph, 0)
-                if s == 8 * (ph + 1) + (lag if ph < 3 else 0):
-                    do_FIN(ph, 1)
-            if 0 <= s + 1 < 32:
-                do_S1(s + 1)
-            for u in range(16):
-                if t_step[u] == s:
-                    do_T(u)
-            if 0 <= s < 32:
-                do_B(s, 0)
-                if lag == 0:
-                    do_B(s, 1)
-            if 0 <= s + 2 < 32:
-                do_R(s + 2)
-            if 0 <= s + 1 < 32:
-                do_QK(s + 1)
-            for u in range(16):
-                if t_step[u] == s - 1:
-                    do_QX(u)
-            if 0 <= s < 32:
-                do_QD(s, 0)
-                do_S2(s, 0)
-            if lag == 0:
-                if 0 <= s < 32:
-                    do_QD(s, 1)
-                    do_S2(s, 1)
-            else:
-                if 0 <= s - 1 < 31:
-                    do_QD(s - 1, 1)
-                    do_S2(s - 1, 1)
-                if 0 <= s < 32:
-                    do_B(s, 1)
-                if s == 31:
-                    do_QD(s, 1)
-                    do_S2(s, 1)
-            for i in range(3, 8):
-                if x_emit[i] == s:
-                    load_x(i)
-            if (s + 7) % 2 == 0 and 4 <= (s + 7) // 2 < 16:
-                load_blk((s + 7) // 2)
+        g_eng = nc.gpsimd if G_SHARE else nc.vector
+        for g in range(0, 17):
+            if 4 <= g + 4 < 16:
+                do_X(g + 4)
+            if g < 16:
+                for ps in range(4):
+                    if g > 0 or ps == 3:
+                        do_A(g, ps)
+            if g >= 2:
+                do_FIN(g - 2)
+            if g == 16:
+                do_FIN(15)
+            if 4 < g + 5 < 16:
+                do_T(g + 5)
+            if g < 16:
+                do_B(g, 0, nc.vector)
+                do_R(g)
+            if 4 <= g + 4 < 16:
+                do_QX(g + 4)
+            if g + 1 < 16:
+                for ps in range(4):
+                    do_S1(g + 1, ps)
+            if 1 <= g < 16:
+                do_QK(g - 1)
+            if g < 16:
+                do_QD(g, 0)
+            if 1 <= g < 16:
+                do_QD(g - 1, 1)
+                do_S2(g - 1)
+            if g < 15:
+                do_B(g, 1, g_eng)
+            if g == 15:
+                do_B(g, 1, nc.vector)
+                do_QK(g)
+                do_QD(g, 1)
+                do_S2(g)
+            for i in range(4, 8):
+                if 2 * i - 8 == g:
+                    load_x(i, 1)
+            for k in range(3, 8):
+                if 2 * k - 5 == g:
+                    load_vo(k, [0, 1])
+            for k in range(3, 8):
+                if 2 * k - 5 == g:
+                    load_k(k)

@@ -26,7 +26,7 @@ def tile_dpfpattention_pb_t_kernel(tc, x, wv, beta, vo, k_phi, W, out):
     nc = tc.nc
     with ExitStack() as ctx:
         const = ctx.enter_context(tc.tile_pool(name="const", bufs=1))
-        xraw_pool = ctx.enter_context(tc.tile_pool(name="xraw", bufs=3))
+        xraw_pool = ctx.enter_context(tc.tile_pool(name="xraw", bufs=4))
         xg_pool = ctx.enter_context(tc.tile_pool(name="xg", bufs=2))
         vo_pool = ctx.enter_context(tc.tile_pool(name="vo", bufs=3))
         kraw_pool = ctx.enter_context(tc.tile_pool(name="kraw", bufs=3))
@@ -35,8 +35,8 @@ def tile_dpfpattention_pb_t_kernel(tc, x, wv, beta, vo, k_phi, W, out):
         kw_pool = ctx.enter_context(tc.tile_pool(name="kw", bufs=2))
         t_pool = ctx.enter_context(tc.tile_pool(name="t", bufs=3))
         dv_pool = ctx.enter_context(tc.tile_pool(name="dv", bufs=2))
-        res_pool = ctx.enter_context(tc.tile_pool(name="res", bufs=2))
-        ps_acc = ctx.enter_context(tc.psum_pool(name="ps_acc", bufs=2))
+        ps_acc = ctx.enter_context(tc.psum_pool(name="ps_acc", bufs=1))
+        ps_bt = ctx.enter_context(tc.psum_pool(name="ps_bt", bufs=1))
         ps_s1 = ctx.enter_context(tc.psum_pool(name="ps_s1", bufs=4))
         ps_xt = ctx.enter_context(tc.psum_pool(name="ps_xt", bufs=2))
         ctx.enter_context(tc.manual_schedule())
@@ -47,6 +47,7 @@ def tile_dpfpattention_pb_t_kernel(tc, x, wv, beta, vo, k_phi, W, out):
         bv = beta.rearrange("b h (d0 c x) -> c (b h) d0 x", d0=D0, c=NC, x=IL * R)
 
         part = const.tile([P, 16, DH], F32)
+        res = const.tile([P, 16, DH], F32)
 
         xraws, voraws, kraws, xws = {}, {}, {}, {}
         xts, xgs, kgs, kws, s1s, ts, dvgs, dvws, accs = {}, {}, {}, {}, {}, {}, {}, {}, {}
@@ -110,8 +111,8 @@ def tile_dpfpattention_pb_t_kernel(tc, x, wv, beta, vo, k_phi, W, out):
             pq = g % 4
             kraw = kraws[g // 2]
             kg = kg_pool.tile([P, 2, 4, S, 4], BF16, name="kg", align_bytes=64)
-            for e in range(2):
-                for ps in range(4):
+            for ps in range(4):
+                for e in range(2):
                     cl, rhi = divmod(ps, 2)
                     nc.scalar.copy(out=kg[:, e, ps].rearrange("p (c i) t -> p c t i", i=4),
                                    in_=kraw[:, cl, 2 * (pq % 2) + e, 4 * rhi:4 * rhi + 4, :].rearrange("p t (c i) -> p c t i", i=4))
@@ -146,10 +147,21 @@ def tile_dpfpattention_pb_t_kernel(tc, x, wv, beta, vo, k_phi, W, out):
                                     op=ALU.subtract)
 
         def do_B(g, half, eng):
+            b, ch, pq = where(g)
             dvg = dv_pool.tile([P, 4, DH, 4], BF16, name="dvg%d" % half, align_bytes=64, bufs=(1 if half == 1 else 2))
-            bb = beta2[:, g, 4 * half:4 * half + 4, :].unsqueeze(2).to_broadcast([P, 4, DH, 4])
-            eng.tensor_tensor(out=dvg[:], in0=ts[g][:, 4 * half:4 * half + 4], in1=bb, op=ALU.mult)
             dvgs[(g, half)] = dvg
+            if eng is None:
+                nc.vector.memset(dvg[:, 0, 0, :], 0.0)
+                return
+            if eng == "g":
+                bb = beta2[:, g, :, :].unsqueeze(2).to_broadcast([P, 4, DH, 4])
+                nc.gpsimd.tensor_tensor(out=dvg[:], in0=ts[g][:, 4 * half:4 * half + 4], in1=bb, op=ALU.mult)
+                return
+            for rhi in range(2):
+                ps = 2 * half + rhi
+                row0 = 16 * (2 * ch + half) + 8 * b + 2 * pq
+                bb = bt[:, 4 * rhi:4 * rhi + 4, row0:row0 + 2].rearrange("p j hh -> p hh j").unsqueeze(2).to_broadcast([P, 2, DH, 4])
+                nc.vector.tensor_tensor(out=dvg[:, 2 * rhi:2 * rhi + 2], in0=ts[g][:, 2 * ps:2 * ps + 2], in1=bb, op=ALU.mult)
 
         def do_QD(g, half):
             dvw = dv_pool.tile([P, 256], U32, name="dvw%d" % half, align_bytes=64)
@@ -179,66 +191,64 @@ def tile_dpfpattention_pb_t_kernel(tc, x, wv, beta, vo, k_phi, W, out):
             if ch == 0:
                 nc.vector.tensor_tensor(out=part[:, h0:h0 + 2, :], in0=valid, in1=w_sb[:, h0:h0 + 2, :], op=ALU.add)
             else:
-                res = res_pool.tile([P, 2, DH], F32, name="res")
-                nc.vector.tensor_tensor(out=res[:], in0=valid, in1=part[:, h0:h0 + 2, :], op=ALU.add)
-                nc.sync.dma_start(out=out[b, 2 * pq:2 * pq + 2].rearrange("h s d -> s h d"), in_=res[:])
+                nc.vector.tensor_tensor(out=res[:, h0:h0 + 2, :], in0=valid, in1=part[:, h0:h0 + 2, :], op=ALU.add)
+                nc.sync.dma_start(out=out[b, 2 * pq:2 * pq + 2].rearrange("h s d -> s h d"), in_=res[:, h0:h0 + 2, :])
 
-        load_x(0, 2)
         wraw = const.tile([P, 4, 512], BF16)
         for w in range(2):
             nc.sync.dma_start(out=wraw[:, 2 * w:2 * w + 2, :], in_=wv[256 * w:256 * w + 256, :].rearrange("(q e) c -> q e c", e=2))
-        bc = const.tile([P, 1024], BF16)
-        nc.vector.memset(bc[64:P, :], 0.0)
-        for c in range(NC):
-            nc.scalar.dma_start(out=bc[16 * c:16 * c + 16, :].rearrange("p (d0 x) -> p d0 x", x=IL * R), in_=bv[c])
-        w_sb = const.tile([P, 16, DH], BF16)
-        nc.scalar.dma_start(out=w_sb[:], in_=W.rearrange("b h s d -> s (b h) d"))
-        ident_b = const.tile([P, P], BF16)
-        make_identity(nc, ident_b[:])
+        load_x(0, 1)
+        load_x(1, 1)
         ident_f = const.tile([P, P], F32)
         make_identity(nc, ident_f[:])
+        ident_b = const.tile([P, P], BF16)
+        make_identity(nc, ident_b[:])
+        bc = const.tile([P, 1024], BF16)
+        nc.vector.memset(bc[64:P, :], 0.0)
         load_vo(0, [0])
-        load_x(1, 1)
         load_vo(0, [1])
-        load_k(0)
+        for c in range(NC):
+            nc.sync.dma_start(out=bc[16 * c:16 * c + 16, :].rearrange("p (d0 x) -> p d0 x", x=IL * R), in_=bv[c])
         load_x(2, 1)
+        load_k(0)
         load_vo(1, [0, 1])
+        load_x(3, 1)
+        w_sb = const.tile([P, 16, DH], BF16)
+        nc.sync.dma_start(out=w_sb[:], in_=W.rearrange("b h s d -> s (b h) d"))
         load_k(1)
-        load_vo(2, [0, 1])
-        load_k(2)
 
-        bt = ps_s1.tile([P, R, P], BF16, name="bt", tag="s1")
-        bcv = bc[:].rearrange("p (q r) -> p q r", r=R)
-        for r in range(R):
-            nc.tensor.transpose(bt[:, r, :], bcv[:, :, r], ident_b[:])
-        beta2 = const.tile([P, 16, 8, 4], F32)
-        for b in range(B):
-            for c in range(NC):
-                ch, cl = divmod(c, 2)
-                for rhi in range(2):
-                    g0 = 8 * b + 4 * ch
-                    q0 = 2 * (2 * cl + rhi)
-                    row0 = 16 * c + 8 * b
-                    nc.scalar.copy(out=beta2[:, g0:g0 + 4, q0:q0 + 2, :],
-                                   in_=bt[:, 4 * rhi:4 * rhi + 4, row0:row0 + 8].rearrange("p j (pq hh) -> p pq hh j", hh=2))
         wgrp = const.tile([P, 512, 4], BF16, align_bytes=64)
         wvw = const.tile([P, 512], U32, align_bytes=64)
         wvs = const.tile([P, 512], U8, align_bytes=64)
         nc.vector.tensor_copy(out=wgrp[:], in_=wraw[:].rearrange("p t c -> p c t"))
         nc.vector.quantize_mx(out=wvw[:].bitcast(FP8X4), scales=wvs[:], in_=wgrp[:].rearrange("p c t -> p (c t)"))
-
+        do_T(0)
+        bt = ps_bt.tile([P, R, P], BF16, name="bt")
+        bcv = bc[:].rearrange("p (q r) -> p q r", r=R)
+        beta2 = const.tile([P, 16, 4, 4], F32)
         for u in range(4):
-            do_T(u)
             do_X(u)
+            if u < 3:
+                do_T(u + 1)
             do_QX(u)
+            if u == 3:
+                for r in range(R):
+                    nc.tensor.transpose(bt[:, r, :], bcv[:, :, r], ident_b[:])
             do_S1(0, u)
             if u > 0:
                 do_A(0, u - 1)
-            if u == 1:
-                load_x(3, 1)
         do_T(4)
+        for b in range(B):
+            for ch in range(2):
+                for rhi in range(2):
+                    g0 = 8 * b + 4 * ch
+                    row0 = 16 * (2 * ch + 1) + 8 * b
+                    nc.vector.tensor_copy(out=beta2[:, g0:g0 + 4, 2 * rhi:2 * rhi + 2, :],
+                                          in_=bt[:, 4 * rhi:4 * rhi + 4, row0:row0 + 8].rearrange("p j (pq hh) -> p pq hh j", hh=2))
+        load_x(4, 1)
+        load_vo(2, [0, 1])
+        load_k(2)
 
-        g_eng = nc.gpsimd if G_SHARE else nc.vector
         for g in range(0, 17):
             if 4 <= g + 4 < 16:
                 do_X(g + 4)
@@ -246,20 +256,20 @@ def tile_dpfpattention_pb_t_kernel(tc, x, wv, beta, vo, k_phi, W, out):
                 for ps in range(4):
                     if g > 0 or ps == 3:
                         do_A(g, ps)
-            if g >= 2:
+            if 2 <= g < 16:
                 do_FIN(g - 2)
             if g == 16:
                 do_FIN(15)
-            if 4 < g + 5 < 16:
-                do_T(g + 5)
             if g < 16:
-                do_B(g, 0, nc.vector)
+                do_B(g, 0, "v")
                 do_R(g)
             if 4 <= g + 4 < 16:
                 do_QX(g + 4)
             if g + 1 < 16:
                 for ps in range(4):
                     do_S1(g + 1, ps)
+            if 4 < g + 5 < 16:
+                do_T(g + 5)
             if 1 <= g < 16:
                 do_QK(g - 1)
             if g < 16:
@@ -268,14 +278,15 @@ def tile_dpfpattention_pb_t_kernel(tc, x, wv, beta, vo, k_phi, W, out):
                 do_QD(g - 1, 1)
                 do_S2(g - 1)
             if g < 15:
-                do_B(g, 1, g_eng)
+                do_B(g, 1, "g" if G_SHARE else "v")
             if g == 15:
-                do_B(g, 1, nc.vector)
+                do_B(g, 1, "v")
                 do_QK(g)
+                do_FIN(g - 1)
                 do_QD(g, 1)
                 do_S2(g)
-            for i in range(4, 8):
-                if 2 * i - 8 == g:
+            for i in range(5, 8):
+                if 2 * i - 9 == g:
                     load_x(i, 1)
             for k in range(3, 8):
                 if 2 * k - 5 == g:

@@ -27,7 +27,7 @@ def tile_dpfpattention_pb_t_kernel(tc, x, wv, beta, vo, k_phi, W, out):
     with ExitStack() as ctx:
         const = ctx.enter_context(tc.tile_pool(name="const", bufs=1))
         xraw_pool = ctx.enter_context(tc.tile_pool(name="xraw", bufs=4))
-        xg_pool = ctx.enter_context(tc.tile_pool(name="xg", bufs=2))
+        xg_pool = ctx.enter_context(tc.tile_pool(name="xg", bufs=3))
         vo_pool = ctx.enter_context(tc.tile_pool(name="vo", bufs=3))
         kraw_pool = ctx.enter_context(tc.tile_pool(name="kraw", bufs=3))
         xw_pool = ctx.enter_context(tc.tile_pool(name="xw", bufs=8))
@@ -55,14 +55,15 @@ def tile_dpfpattention_pb_t_kernel(tc, x, wv, beta, vo, k_phi, W, out):
         def where(g):
             return g // 8, (g // 4) % 2, g % 4
 
-        def load_x(i, pieces):
+        def load_x(i, pieces, which):
             b, c = divmod(i, NC)
-            xraw = xraw_pool.tile([P, R, D], BF16, name="xraw")
+            if i not in xraws:
+                xraws[i] = xraw_pool.tile([P, R, D], BF16, name="xraw")
+            xraw = xraws[i]
             n = R // pieces
-            for q in range(pieces):
+            for q in which:
                 for il in range(IL):
                     nc.sync.dma_start(out=xraw[il:P:IL, n * q:n * q + n, :], in_=xv[b, c, il][:, n * q:n * q + n, :])
-            xraws[i] = xraw
 
         def load_vo(k, cls):
             b, ch, hf = k // 4, (k // 2) % 2, k % 2
@@ -146,28 +147,31 @@ def tile_dpfpattention_pb_t_kernel(tc, x, wv, beta, vo, k_phi, W, out):
                                     in1=voraws[g // 2][:, cl, h0:h0 + 2, 4 * rhi:4 * rhi + 4, :].rearrange("p hh j d -> p hh d j"),
                                     op=ALU.subtract)
 
-        def do_B(g, half, eng):
-            b, ch, pq = where(g)
-            dvg = dv_pool.tile([P, 4, DH, 4], BF16, name="dvg%d" % half, align_bytes=64, bufs=(1 if half == 1 else 2))
-            dvgs[(g, half)] = dvg
-            if eng is None:
-                nc.vector.memset(dvg[:, 0, 0, :], 0.0)
-                return
-            if eng == "g":
-                bb = beta2[:, g, :, :].unsqueeze(2).to_broadcast([P, 4, DH, 4])
-                nc.gpsimd.tensor_tensor(out=dvg[:], in0=ts[g][:, 4 * half:4 * half + 4], in1=bb, op=ALU.mult)
-                return
-            for rhi in range(2):
-                ps = 2 * half + rhi
-                row0 = 16 * (2 * ch + half) + 8 * b + 2 * pq
-                bb = bt[:, 4 * rhi:4 * rhi + 4, row0:row0 + 2].rearrange("p j hh -> p hh j").unsqueeze(2).to_broadcast([P, 2, DH, 4])
-                nc.vector.tensor_tensor(out=dvg[:, 2 * rhi:2 * rhi + 2], in0=ts[g][:, 2 * ps:2 * ps + 2], in1=bb, op=ALU.mult)
+        PARTS = {"a": (0, 2), "b": (2, 6)}
 
-        def do_QD(g, half):
-            dvw = dv_pool.tile([P, 256], U32, name="dvw%d" % half, align_bytes=64)
-            dvs = dv_pool.tile([P, 256], U8, name="dvs%d" % half, align_bytes=64)
-            nc.vector.quantize_mx(out=dvw[:].bitcast(FP8X4), scales=dvs[:], in_=dvgs[(g, half)][:].rearrange("p q d j -> p (q d j)"))
-            dvws[(g, half)] = (dvw, dvs)
+        def new_dv(g, part):
+            n = PARTS[part][1]
+            dvgs[(g, part)] = dv_pool.tile([P, n, DH, 4], BF16, name="dvg" + part, align_bytes=64, bufs=(2 if part == "a" else 1))
+
+        def do_Bv(g, part, u0, n):
+            b, ch, pq = where(g)
+            first = PARTS[part][0]
+            ps, hh0 = divmod(u0, 2)
+            cl, rhi = divmod(ps, 2)
+            row0 = 16 * (2 * ch + cl) + 8 * b + 2 * pq + hh0
+            bb = bt[:, 4 * rhi:4 * rhi + 4, row0:row0 + n].rearrange("p j hh -> p hh j").unsqueeze(2).to_broadcast([P, n, DH, 4])
+            nc.vector.tensor_tensor(out=dvgs[(g, part)][:, u0 - first:u0 - first + n], in0=ts[g][:, u0:u0 + n], in1=bb, op=ALU.mult)
+
+        def do_Bg(g, part, u0, n):
+            first = PARTS[part][0]
+            bb = beta2[:, g, u0:u0 + n, :].unsqueeze(2).to_broadcast([P, n, DH, 4])
+            nc.gpsimd.tensor_tensor(out=dvgs[(g, part)][:, u0 - first:u0 - first + n], in0=ts[g][:, u0:u0 + n], in1=bb, op=ALU.mult)
+
+        def do_QD(g, part, key, u0, n):
+            dvw = dv_pool.tile([P, n * DH], U32, name="dvw" + key, align_bytes=64)
+            dvs = dv_pool.tile([P, n * DH], U8, name="dvs" + key, align_bytes=64)
+            nc.vector.quantize_mx(out=dvw[:].bitcast(FP8X4), scales=dvs[:], in_=dvgs[(g, part)][:, u0:u0 + n].rearrange("p q d j -> p (q d j)"))
+            dvws[(g, key)] = (dvw, dvs)
 
         def do_S2(g):
             kw, ks = kws[g]
@@ -175,9 +179,9 @@ def tile_dpfpattention_pb_t_kernel(tc, x, wv, beta, vo, k_phi, W, out):
             av = acc[:].rearrange("p (e q) d -> p e (q d)", e=2)
             for e in range(2):
                 for ps in range(4):
-                    dvw, dvs = dvws[(g, ps // 2)]
+                    dvw, dvs = dvws[(g, "abcc"[ps])]
                     o = (4 * e + ps) * P
-                    r0 = P * (ps % 2)
+                    r0 = P if ps == 3 else 0
                     nc.tensor.matmul_mx(out=av[:, e, :],
                                         lhsT=kw[:, o:o + P].bitcast(FP8X4), lhsT_scale=ks[:, o:o + P],
                                         rhs=dvw[:, r0:r0 + P].bitcast(FP8X4), rhs_scale=dvs[:, r0:r0 + P],
@@ -194,11 +198,12 @@ def tile_dpfpattention_pb_t_kernel(tc, x, wv, beta, vo, k_phi, W, out):
                 nc.vector.tensor_tensor(out=res[:, h0:h0 + 2, :], in0=valid, in1=part[:, h0:h0 + 2, :], op=ALU.add)
                 nc.sync.dma_start(out=out[b, 2 * pq:2 * pq + 2].rearrange("h s d -> s h d"), in_=res[:, h0:h0 + 2, :])
 
+        load_x(0, 2, [0])
         wraw = const.tile([P, 4, 512], BF16)
         for w in range(2):
             nc.sync.dma_start(out=wraw[:, 2 * w:2 * w + 2, :], in_=wv[256 * w:256 * w + 256, :].rearrange("(q e) c -> q e c", e=2))
-        load_x(0, 1)
-        load_x(1, 1)
+        load_x(0, 2, [1])
+        load_x(1, 1, [0])
         ident_f = const.tile([P, P], F32)
         make_identity(nc, ident_f[:])
         ident_b = const.tile([P, P], BF16)
@@ -209,10 +214,10 @@ def tile_dpfpattention_pb_t_kernel(tc, x, wv, beta, vo, k_phi, W, out):
         load_vo(0, [1])
         for c in range(NC):
             nc.sync.dma_start(out=bc[16 * c:16 * c + 16, :].rearrange("p (d0 x) -> p d0 x", x=IL * R), in_=bv[c])
-        load_x(2, 1)
+        load_x(2, 1, [0])
         load_k(0)
         load_vo(1, [0, 1])
-        load_x(3, 1)
+        load_x(3, 1, [0])
         w_sb = const.tile([P, 16, DH], BF16)
         nc.sync.dma_start(out=w_sb[:], in_=W.rearrange("b h s d -> s (b h) d"))
         load_k(1)
@@ -220,12 +225,16 @@ def tile_dpfpattention_pb_t_kernel(tc, x, wv, beta, vo, k_phi, W, out):
         wgrp = const.tile([P, 512, 4], BF16, align_bytes=64)
         wvw = const.tile([P, 512], U32, align_bytes=64)
         wvs = const.tile([P, 512], U8, align_bytes=64)
-        nc.vector.tensor_copy(out=wgrp[:], in_=wraw[:].rearrange("p t c -> p c t"))
-        nc.vector.quantize_mx(out=wvw[:].bitcast(FP8X4), scales=wvs[:], in_=wgrp[:].rearrange("p c t -> p (c t)"))
+
+        def prep_wv(c0, c1):
+            nc.vector.tensor_copy(out=wgrp[:, c0:c1, :], in_=wraw[:, :, c0:c1].rearrange("p t c -> p c t"))
+            nc.vector.quantize_mx(out=wvw[:, c0:c1].bitcast(FP8X4), scales=wvs[:, c0:c1], in_=wgrp[:, c0:c1, :].rearrange("p c t -> p (c t)"))
+
+        prep_wv(0, P)
         do_T(0)
         bt = ps_bt.tile([P, R, P], BF16, name="bt")
         bcv = bc[:].rearrange("p (q r) -> p q r", r=R)
-        beta2 = const.tile([P, 16, 4, 4], F32)
+        beta2 = const.tile([P, 16, 8, 4], F32)
         for u in range(4):
             do_X(u)
             if u < 3:
@@ -235,22 +244,33 @@ def tile_dpfpattention_pb_t_kernel(tc, x, wv, beta, vo, k_phi, W, out):
                 for r in range(R):
                     nc.tensor.transpose(bt[:, r, :], bcv[:, :, r], ident_b[:])
             do_S1(0, u)
+            if u == 0:
+                prep_wv(P, 2 * P)
+                prep_wv(2 * P, 4 * P)
             if u > 0:
                 do_A(0, u - 1)
         do_T(4)
+        do_X(4)
+        do_T(5)
         for b in range(B):
-            for ch in range(2):
+            for c in range(NC):
                 for rhi in range(2):
+                    if c % 2 == 0 and rhi == 0:
+                        continue
+                    ch, cl = divmod(c, 2)
                     g0 = 8 * b + 4 * ch
-                    row0 = 16 * (2 * ch + 1) + 8 * b
-                    nc.vector.tensor_copy(out=beta2[:, g0:g0 + 4, 2 * rhi:2 * rhi + 2, :],
+                    q0 = 2 * (2 * cl + rhi)
+                    row0 = 16 * c + 8 * b
+                    nc.vector.tensor_copy(out=beta2[:, g0:g0 + 4, q0:q0 + 2, :],
                                           in_=bt[:, 4 * rhi:4 * rhi + 4, row0:row0 + 8].rearrange("p j (pq hh) -> p pq hh j", hh=2))
-        load_x(4, 1)
+        load_x(4, 1, [0])
         load_vo(2, [0, 1])
         load_k(2)
 
         for g in range(0, 17):
-            if 4 <= g + 4 < 16:
+            if g == 0:
+                do_X(5)
+            if 6 <= g + 4 < 16:
                 do_X(g + 4)
             if g < 16:
                 for ps in range(4):
@@ -261,33 +281,42 @@ def tile_dpfpattention_pb_t_kernel(tc, x, wv, beta, vo, k_phi, W, out):
             if g == 16:
                 do_FIN(15)
             if g < 16:
-                do_B(g, 0, "v")
+                new_dv(g, "a")
+                do_Bv(g, "a", 0, 2)
+                if g >= 1:
+                    do_Bv(g - 1, "b", 2, 1)
                 do_R(g)
             if 4 <= g + 4 < 16:
                 do_QX(g + 4)
             if g + 1 < 16:
                 for ps in range(4):
                     do_S1(g + 1, ps)
-            if 4 < g + 5 < 16:
+            if 6 <= g + 5 < 16:
                 do_T(g + 5)
             if 1 <= g < 16:
                 do_QK(g - 1)
             if g < 16:
-                do_QD(g, 0)
+                do_QD(g, "a", "a", 0, 2)
             if 1 <= g < 16:
-                do_QD(g - 1, 1)
+                do_QD(g - 1, "b", "b", 0, 2)
+                do_QD(g - 1, "b", "c", 2, 4)
                 do_S2(g - 1)
+            if g < 16:
+                new_dv(g, "b")
             if g < 15:
-                do_B(g, 1, "g" if G_SHARE else "v")
+                do_Bg(g, "b", 3, 5)
             if g == 15:
-                do_B(g, 1, "v")
+                do_Bv(g, "b", 2, 2)
+                do_Bv(g, "b", 4, 2)
+                do_Bv(g, "b", 6, 2)
                 do_QK(g)
                 do_FIN(g - 1)
-                do_QD(g, 1)
+                do_QD(g, "b", "b", 0, 2)
+                do_QD(g, "b", "c", 2, 4)
                 do_S2(g)
             for i in range(5, 8):
                 if 2 * i - 9 == g:
-                    load_x(i, 1)
+                    load_x(i, 1, [0])
             for k in range(3, 8):
                 if 2 * k - 5 == g:
                     load_vo(k, [0, 1])

@@ -147,31 +147,30 @@ def tile_dpfpattention_pb_t_kernel(tc, x, wv, beta, vo, k_phi, W, out):
                                     in1=voraws[g // 2][:, cl, h0:h0 + 2, 4 * rhi:4 * rhi + 4, :].rearrange("p hh j d -> p hh d j"),
                                     op=ALU.subtract)
 
-        PARTS = {"a": (0, 2), "b": (2, 6)}
+        def new_dv(g):
+            dvgs[g] = dv_pool.tile([P, 8, DH, 4], BF16, name="dvg", align_bytes=64, bufs=1)
 
-        def new_dv(g, part):
-            n = PARTS[part][1]
-            dvgs[(g, part)] = dv_pool.tile([P, n, DH, 4], BF16, name="dvg" + part, align_bytes=64, bufs=(2 if part == "a" else 1))
-
-        def do_Bv(g, part, u0, n):
+        def do_Bv(g, u0, n):
             b, ch, pq = where(g)
-            first = PARTS[part][0]
             ps, hh0 = divmod(u0, 2)
             cl, rhi = divmod(ps, 2)
             row0 = 16 * (2 * ch + cl) + 8 * b + 2 * pq + hh0
             bb = bt[:, 4 * rhi:4 * rhi + 4, row0:row0 + n].rearrange("p j hh -> p hh j").unsqueeze(2).to_broadcast([P, n, DH, 4])
-            nc.vector.tensor_tensor(out=dvgs[(g, part)][:, u0 - first:u0 - first + n], in0=ts[g][:, u0:u0 + n], in1=bb, op=ALU.mult)
+            dst = dvgs[g if ps == 0 else g + 1]
+            nc.vector.tensor_tensor(out=dst[:, u0:u0 + n], in0=ts[g][:, u0:u0 + n], in1=bb, op=ALU.mult)
 
-        def do_Bg(g, part, u0, n):
-            first = PARTS[part][0]
+        def do_Bg(g, u0, n):
             bb = beta2[:, g, u0:u0 + n, :].unsqueeze(2).to_broadcast([P, n, DH, 4])
-            nc.gpsimd.tensor_tensor(out=dvgs[(g, part)][:, u0 - first:u0 - first + n], in0=ts[g][:, u0:u0 + n], in1=bb, op=ALU.mult)
+            nc.gpsimd.tensor_tensor(out=dvgs[g + 1][:, u0:u0 + n], in0=ts[g][:, u0:u0 + n], in1=bb, op=ALU.mult)
 
-        def do_QD(g, part, key, u0, n):
-            dvw = dv_pool.tile([P, n * DH], U32, name="dvw" + key, align_bytes=64)
-            dvs = dv_pool.tile([P, n * DH], U8, name="dvs" + key, align_bytes=64)
-            nc.vector.quantize_mx(out=dvw[:].bitcast(FP8X4), scales=dvs[:], in_=dvgs[(g, part)][:, u0:u0 + n].rearrange("p q d j -> p (q d j)"))
-            dvws[(g, key)] = (dvw, dvs)
+        def do_QD(g, u0, n):
+            if g not in dvws:
+                dvw = dv_pool.tile([P, 8 * DH], U32, name="dvw", align_bytes=64, bufs=3)
+                dvs = dv_pool.tile([P, 8 * DH], U8, name="dvs", align_bytes=64, bufs=3)
+                dvws[g] = (dvw, dvs)
+            dvw, dvs = dvws[g]
+            nc.vector.quantize_mx(out=dvw[:, DH * u0:DH * (u0 + n)].bitcast(FP8X4), scales=dvs[:, DH * u0:DH * (u0 + n)],
+                                  in_=dvgs[g][:, u0:u0 + n].rearrange("p q d j -> p (q d j)"))
 
         def do_S2(g):
             kw, ks = kws[g]
@@ -179,9 +178,9 @@ def tile_dpfpattention_pb_t_kernel(tc, x, wv, beta, vo, k_phi, W, out):
             av = acc[:].rearrange("p (e q) d -> p e (q d)", e=2)
             for e in range(2):
                 for ps in range(4):
-                    dvw, dvs = dvws[(g, "abcc"[ps])]
+                    dvw, dvs = dvws[g if ps == 0 else g + 1]
                     o = (4 * e + ps) * P
-                    r0 = P if ps == 3 else 0
+                    r0 = P * ps
                     nc.tensor.matmul_mx(out=av[:, e, :],
                                         lhsT=kw[:, o:o + P].bitcast(FP8X4), lhsT_scale=ks[:, o:o + P],
                                         rhs=dvw[:, r0:r0 + P].bitcast(FP8X4), rhs_scale=dvs[:, r0:r0 + P],
@@ -281,10 +280,11 @@ def tile_dpfpattention_pb_t_kernel(tc, x, wv, beta, vo, k_phi, W, out):
             if g == 16:
                 do_FIN(15)
             if g < 16:
-                new_dv(g, "a")
-                do_Bv(g, "a", 0, 2)
+                if g == 0:
+                    new_dv(0)
+                do_Bv(g, 0, 2)
                 if g >= 1:
-                    do_Bv(g - 1, "b", 2, 1)
+                    do_Bv(g - 1, 2, 1)
                 do_R(g)
             if 4 <= g + 4 < 16:
                 do_QX(g + 4)
@@ -295,24 +295,23 @@ def tile_dpfpattention_pb_t_kernel(tc, x, wv, beta, vo, k_phi, W, out):
                 do_T(g + 5)
             if 1 <= g < 16:
                 do_QK(g - 1)
-            if g < 16:
-                do_QD(g, "a", "a", 0, 2)
+            if g == 0:
+                do_QD(0, 0, 2)
             if 1 <= g < 16:
-                do_QD(g - 1, "b", "b", 0, 2)
-                do_QD(g - 1, "b", "c", 2, 4)
+                do_QD(g, 0, 8)
                 do_S2(g - 1)
             if g < 16:
-                new_dv(g, "b")
+                new_dv(g + 1)
             if g < 15:
-                do_Bg(g, "b", 3, 5)
+                do_Bg(g, 3, 5)
             if g == 15:
-                do_Bv(g, "b", 2, 2)
-                do_Bv(g, "b", 4, 2)
-                do_Bv(g, "b", 6, 2)
+                do_Bv(g, 2, 2)
+                do_Bv(g, 4, 2)
+                do_Bv(g, 6, 2)
                 do_QK(g)
                 do_FIN(g - 1)
-                do_QD(g, "b", "b", 0, 2)
-                do_QD(g, "b", "c", 2, 4)
+                do_QD(g + 1, 2, 2)
+                do_QD(g + 1, 4, 4)
                 do_S2(g)
             for i in range(5, 8):
                 if 2 * i - 9 == g:

@@ -50,7 +50,7 @@ def tile_dpfpattention_pb_t_kernel(tc, x, wv, beta, vo, k_phi, W, out):
         res = const.tile([P, 16, DH], F32)
 
         xraws, voraws, kraws, xws = {}, {}, {}, {}
-        xts, xgs, kgs, kws, s1s, ts, dvgs, dvws, accs = {}, {}, {}, {}, {}, {}, {}, {}, {}
+        xts, xgs, kgs, kws, s1s, ts, dvgs, dvws, accs, kts = {}, {}, {}, {}, {}, {}, {}, {}, {}, {}
 
         def where(g):
             return g // 8, (g // 4) % 2, g % 4
@@ -113,11 +113,23 @@ def tile_dpfpattention_pb_t_kernel(tc, x, wv, beta, vo, k_phi, W, out):
             kraw = kraws[g // 2]
             kg = kg_pool.tile([P, 2, 4, S, 4], BF16, name="kg", align_bytes=64)
             for ps in range(4):
+                if ps == 1:
+                    nc.scalar.copy(out=kg[:, :, 3].rearrange("p e s j -> p e (s j)"), in_=kts[g][:])
+                if ps == 3:
+                    continue
                 for e in range(2):
                     cl, rhi = divmod(ps, 2)
                     nc.scalar.copy(out=kg[:, e, ps].rearrange("p (c i) t -> p c t i", i=4),
                                    in_=kraw[:, cl, 2 * (pq % 2) + e, 4 * rhi:4 * rhi + 4, :].rearrange("p t (c i) -> p c t i", i=4))
             kgs[g] = kg
+
+        def do_KT(g):
+            kt = ps_xt.tile([P, 2, 4 * S], BF16, name="kt", tag="xt")
+            for e in range(2):
+                nc.tensor.matmul(out=kt[:, e, :], lhsT=ident_b[:],
+                                 rhs=kraws[g // 2][:, 1, 2 * (g % 2) + e, 4:8, :].rearrange("p t s -> p s t"),
+                                 start=True, stop=True)
+            kts[g] = kt
 
         def do_QK(g):
             kw = kw_pool.tile([P, 1024], U32, name="kw", align_bytes=64)
@@ -285,6 +297,7 @@ def tile_dpfpattention_pb_t_kernel(tc, x, wv, beta, vo, k_phi, W, out):
                 do_Bv(g, 0, 2)
                 if g >= 1:
                     do_Bv(g - 1, 2, 1)
+                do_KT(g)
                 do_R(g)
             if 4 <= g + 4 < 16:
                 do_QX(g + 4)

@@ -126,8 +126,8 @@ def tile_dpfpattention_pb_t_kernel(tc, x, wv, beta, vo, k_phi, W, out):
         def do_KT(g):
             kt = ps_xt.tile([P, 2, 4 * S], BF16, name="kt", tag="xt")
             for e in range(2):
-                nc.tensor.matmul(out=kt[:, e, :], lhsT=ident_b[:],
-                                 rhs=kraws[g // 2][:, 1, 2 * (g % 2) + e, 4:8, :].rearrange("p t s -> p s t"),
+                nc.tensor.matmul(out=kt[:, e, :].rearrange("p (s t) -> p t s", t=4), lhsT=ident_b[:],
+                                 rhs=kraws[g // 2][:, 1, 2 * (g % 2) + e, 4:8, :],
                                  start=True, stop=True)
             kts[g] = kt
 

@@ -1,8 +1,6 @@
 from contextlib import ExitStack
 
-import concourse.bass as bass
 import concourse.mybir as mybir
-import concourse.tile as tile
 from concourse.masks import make_identity
 
 FP8X4 = mybir.dt.float8_e4m3fn_x4
@@ -16,91 +14,71 @@ B, N, D, H, DH, S = 2, 4096, 512, 8, 64, 128
 P = 128
 FLOPS = 2 * B * N * D * (H * DH) + 2 * B * H * N * S * DH
 
-D0, NC, IL, R = 32, 4, 4, 8
-
-
-G_SHARE = True
+NQ = 8
+STEPS = 16
 
 
 def tile_dpfpattention_pb_t_kernel(tc, x, wv, beta, vo, k_phi, W, out):
     nc = tc.nc
     with ExitStack() as ctx:
         const = ctx.enter_context(tc.tile_pool(name="const", bufs=1))
-        xraw_pool = ctx.enter_context(tc.tile_pool(name="xraw", bufs=4))
+        x_pool = ctx.enter_context(tc.tile_pool(name="x", bufs=8))
         xg_pool = ctx.enter_context(tc.tile_pool(name="xg", bufs=3))
-        vo_pool = ctx.enter_context(tc.tile_pool(name="vo", bufs=3))
-        kraw_pool = ctx.enter_context(tc.tile_pool(name="kraw", bufs=3))
+        vo_pool = ctx.enter_context(tc.tile_pool(name="vo", bufs=6))
+        k_pool = ctx.enter_context(tc.tile_pool(name="k", bufs=6))
         xw_pool = ctx.enter_context(tc.tile_pool(name="xw", bufs=8))
         kg_pool = ctx.enter_context(tc.tile_pool(name="kg", bufs=2))
         kw_pool = ctx.enter_context(tc.tile_pool(name="kw", bufs=2))
         t_pool = ctx.enter_context(tc.tile_pool(name="t", bufs=3))
-        dv_pool = ctx.enter_context(tc.tile_pool(name="dv", bufs=2))
-        ps_acc = ctx.enter_context(tc.psum_pool(name="ps_acc", bufs=1))
-        ps_bt = ctx.enter_context(tc.psum_pool(name="ps_bt", bufs=1))
+        dv_pool = ctx.enter_context(tc.tile_pool(name="dv", bufs=1))
+        ps_bank = ctx.enter_context(tc.psum_pool(name="ps_bank", bufs=1))
         ps_s1 = ctx.enter_context(tc.psum_pool(name="ps_s1", bufs=4))
-        ps_xt = ctx.enter_context(tc.psum_pool(name="ps_xt", bufs=2))
+        ps_xt = ctx.enter_context(tc.psum_pool(name="ps_xt", bufs=3))
         ctx.enter_context(tc.manual_schedule())
 
-        xv = x.rearrange("b (d0 c il r) k -> b c il d0 r k", d0=D0, c=NC, il=IL, r=R)
-        vv = vo.rearrange("b h (d0 c il r) d -> b c il d0 h (r d)", d0=D0, c=NC, il=IL, r=R)
-        kv = k_phi.rearrange("b h (d0 c il r) s -> b c il d0 h (r s)", d0=D0, c=NC, il=IL, r=R)
-        bv = beta.rearrange("b h (d0 c x) -> c (b h) d0 x", d0=D0, c=NC, x=IL * R)
+        xv = x.rearrange("b (q p j) k -> b q p j k", p=P, j=4)
+        vv = vo.rearrange("b h (q p j) d -> b h p q (j d)", p=P, j=4)
+        kv = k_phi.rearrange("b h (q p j) s -> b h p q (j s)", p=P, j=4)
 
         part = const.tile([P, 16, DH], F32)
         res = const.tile([P, 16, DH], F32)
-
         xraws, voraws, kraws, xws = {}, {}, {}, {}
-        xts, xgs, kgs, kws, s1s, ts, dvgs, dvws, accs, kts = {}, {}, {}, {}, {}, {}, {}, {}, {}, {}
+        xts, xgs, kts, kgs, kws, s1s, ts, dvgs, dvws = {}, {}, {}, {}, {}, {}, {}, {}, {}
 
         def where(g):
             return g // 8, (g // 4) % 2, g % 4
 
-        def load_x(i, pieces, which):
-            b, c = divmod(i, NC)
-            if i not in xraws:
-                xraws[i] = xraw_pool.tile([P, R, D], BF16, name="xraw")
-            xraw = xraws[i]
-            n = R // pieces
-            for q in which:
-                for il in range(IL):
-                    nc.sync.dma_start(out=xraw[il:P:IL, n * q:n * q + n, :], in_=xv[b, c, il][:, n * q:n * q + n, :])
+        def load_x(u):
+            xraws[u] = x_pool.tile([P, 4, D], BF16, name="xraw")
+            nc.sync.dma_start(out=xraws[u][:], in_=xv[u // NQ, u % NQ])
 
-        def load_vo(k, cls):
-            b, ch, hf = k // 4, (k // 2) % 2, k % 2
-            if k not in voraws:
-                voraws[k] = vo_pool.tile([P, 2, 4, R, DH], BF16, name="voraw")
-            for cl in cls:
-                for il in range(IL):
-                    nc.sync.dma_start(out=voraws[k][il:P:IL, cl].rearrange("p h r d -> p h (r d)"),
-                                      in_=vv[b, 2 * ch + cl, il][:, 4 * hf:4 * hf + 4, :])
+        def load_vo(g):
+            b, ch, pq = where(g)
+            voraws[g] = vo_pool.tile([P, 2, 4, 4, DH], BF16, name="voraw")
+            for e in range(2):
+                nc.sync.dma_start(out=voraws[g][:, e].rearrange("p q j d -> p q (j d)"), in_=vv[b, 2 * pq + e][:, 4 * ch:4 * ch + 4, :])
 
-        def load_k(k):
-            b, ch, hf = k // 4, (k // 2) % 2, k % 2
-            kraw = kraw_pool.tile([P, 2, 4, R, S], BF16, name="kraw")
-            for cl in range(2):
-                for il in range(IL):
-                    nc.sync.dma_start(out=kraw[il:P:IL, cl].rearrange("p h r s -> p h (r s)"),
-                                      in_=kv[b, 2 * ch + cl, il][:, 4 * hf:4 * hf + 4, :])
-            kraws[k] = kraw
+        def load_k(g):
+            b, ch, pq = where(g)
+            kraws[g] = k_pool.tile([P, 2, 4, 4, S], BF16, name="kraw")
+            for e in range(2):
+                nc.sync.dma_start(out=kraws[g][:, e].rearrange("p q j s -> p q (j s)"), in_=kv[b, 2 * pq + e][:, 4 * ch:4 * ch + 4, :])
 
         def do_T(u):
-            x32 = xraws[u // 2][:].bitcast(F32)
-            rhi = u % 2
-            banks = []
+            x32 = xraws[u][:].bitcast(F32)
+            xts[u] = []
             for jp in range(2):
                 xt = ps_xt.tile([P, 2, 2, P], F32, name="xt", tag="xt")
                 for jl in range(2):
                     for w in range(2):
-                        nc.tensor.transpose(xt[:, jl, w, :], x32[:, 4 * rhi + 2 * jp + jl, P * w:P * w + P], ident_f[:])
-                banks.append(xt)
-            xts[u] = banks
+                        nc.tensor.transpose(xt[:, jl, w, :], x32[:, 2 * jp + jl, P * w:P * w + P], ident_f[:])
+                xts[u].append(xt)
 
         def do_X(u):
-            xg = xg_pool.tile([P, 4, P, 4], BF16, name="xg", align_bytes=64)
-            xg32 = xg[:].bitcast(F32)
+            xgs[u] = xg_pool.tile([P, 4, P, 4], BF16, name="xg", align_bytes=64)
+            xg32 = xgs[u][:].bitcast(F32)
             for jp in range(2):
                 nc.scalar.copy(out=xg32[:, 2 * jp:2 * jp + 2, :, :], in_=xts[u][jp][:].rearrange("p jl w m -> p jl m w"))
-            xgs[u] = xg
 
         def do_QX(u):
             xw = xw_pool.tile([P, 512], U32, name="xw", align_bytes=64)
@@ -108,28 +86,22 @@ def tile_dpfpattention_pb_t_kernel(tc, x, wv, beta, vo, k_phi, W, out):
             nc.vector.quantize_mx(out=xw[:].bitcast(FP8X4), scales=xs[:], in_=xgs[u][:].rearrange("p j m t -> p (j m t)"))
             xws[u] = (xw, xs)
 
-        def do_R(g):
-            pq = g % 4
-            kraw = kraws[g // 2]
-            kg = kg_pool.tile([P, 2, 4, S, 4], BF16, name="kg", align_bytes=64)
-            for ps in range(4):
-                if ps == 1:
-                    nc.scalar.copy(out=kg[:, :, 3].rearrange("p e s j -> p e (s j)"), in_=kts[g][:])
-                if ps == 3:
+        def do_KT(g):
+            kts[g] = ps_xt.tile([P, 2, 4 * S], BF16, name="kt", tag="xt")
+            for e in range(2):
+                nc.tensor.matmul(out=kts[g][:, e, :].rearrange("p (s j) -> p j s", j=4), lhsT=ident_b[:],
+                                 rhs=kraws[g][:, e, 3], start=True, stop=True)
+
+        def do_R(g, pss):
+            if g not in kgs:
+                kgs[g] = kg_pool.tile([P, 2, 4, S, 4], BF16, name="kg", align_bytes=64)
+            for ps in pss:
+                if ps == 3 and g in kts:
+                    nc.scalar.copy(out=kgs[g][:, :, 3].rearrange("p e s j -> p e (s j)"), in_=kts[g][:])
                     continue
                 for e in range(2):
-                    cl, rhi = divmod(ps, 2)
-                    nc.scalar.copy(out=kg[:, e, ps].rearrange("p (c i) t -> p c t i", i=4),
-                                   in_=kraw[:, cl, 2 * (pq % 2) + e, 4 * rhi:4 * rhi + 4, :].rearrange("p t (c i) -> p c t i", i=4))
-            kgs[g] = kg
-
-        def do_KT(g):
-            kt = ps_xt.tile([P, 2, 4 * S], BF16, name="kt", tag="xt")
-            for e in range(2):
-                nc.tensor.matmul(out=kt[:, e, :].rearrange("p (s t) -> p t s", t=4), lhsT=ident_b[:],
-                                 rhs=kraws[g // 2][:, 1, 2 * (g % 2) + e, 4:8, :],
-                                 start=True, stop=True)
-            kts[g] = kt
+                    nc.scalar.copy(out=kgs[g][:, e, ps].rearrange("p (c i) j -> p c j i", i=4),
+                                   in_=kraws[g][:, e, ps].rearrange("p j (c i) -> p c j i", i=4))
 
         def do_QK(g):
             kw = kw_pool.tile([P, 1024], U32, name="kw", align_bytes=64)
@@ -149,25 +121,21 @@ def tile_dpfpattention_pb_t_kernel(tc, x, wv, beta, vo, k_phi, W, out):
             s1s[(g, ps)] = s1
 
         def do_A(g, ps):
-            pq = g % 4
-            cl, rhi = divmod(ps, 2)
             if ps == 0:
                 ts[g] = t_pool.tile([P, 8, DH, 4], F32, name="t")
-            h0 = 2 * (pq % 2)
             nc.vector.tensor_tensor(out=ts[g][:, 2 * ps:2 * ps + 2],
                                     in0=s1s[(g, ps)][:].rearrange("p j (hh d) -> p hh d j", hh=2),
-                                    in1=voraws[g // 2][:, cl, h0:h0 + 2, 4 * rhi:4 * rhi + 4, :].rearrange("p hh j d -> p hh d j"),
+                                    in1=voraws[g][:, :, ps].rearrange("p hh j d -> p hh d j"),
                                     op=ALU.subtract)
 
         def new_dv(g):
-            dvgs[g] = dv_pool.tile([P, 8, DH, 4], BF16, name="dvg", align_bytes=64, bufs=1)
+            dvgs[g] = dv_pool.tile([P, 8, DH, 4], BF16, name="dvg", tag="last" if g == STEPS else "dvg", align_bytes=64)
 
         def do_Bv(g, u0, n):
             b, ch, pq = where(g)
             ps, hh0 = divmod(u0, 2)
-            cl, rhi = divmod(ps, 2)
-            row0 = 16 * (2 * ch + cl) + 8 * b + 2 * pq + hh0
-            bb = bt[:, 4 * rhi:4 * rhi + 4, row0:row0 + n].rearrange("p j hh -> p hh j").unsqueeze(2).to_broadcast([P, n, DH, 4])
+            h0 = 8 * b + 2 * pq + hh0
+            bb = bt[:, :, h0:h0 + n, 4 * ch + ps].rearrange("p j hh -> p hh j").unsqueeze(2).to_broadcast([P, n, DH, 4])
             dst = dvgs[g if ps == 0 else g + 1]
             nc.vector.tensor_tensor(out=dst[:, u0:u0 + n], in0=ts[g][:, u0:u0 + n], in1=bb, op=ALU.mult)
 
@@ -186,52 +154,53 @@ def tile_dpfpattention_pb_t_kernel(tc, x, wv, beta, vo, k_phi, W, out):
 
         def do_S2(g):
             kw, ks = kws[g]
-            acc = ps_acc.tile([P, 4, DH], F32, name="acc", tag="acc")
-            av = acc[:].rearrange("p (e q) d -> p e (q d)", e=2)
             for e in range(2):
                 for ps in range(4):
                     dvw, dvs = dvws[g if ps == 0 else g + 1]
                     o = (4 * e + ps) * P
-                    r0 = P * ps
-                    nc.tensor.matmul_mx(out=av[:, e, :],
+                    nc.tensor.matmul_mx(out=acc[:, P * e:P * e + P],
                                         lhsT=kw[:, o:o + P].bitcast(FP8X4), lhsT_scale=ks[:, o:o + P],
-                                        rhs=dvw[:, r0:r0 + P].bitcast(FP8X4), rhs_scale=dvs[:, r0:r0 + P],
+                                        rhs=dvw[:, P * ps:P * ps + P].bitcast(FP8X4), rhs_scale=dvs[:, P * ps:P * ps + P],
                                         start=(ps == 0), stop=(ps == 3))
-            accs[g] = acc
 
         def do_FIN(g):
             b, ch, pq = where(g)
             h0 = 8 * b + 2 * pq
-            valid = accs[g][:, 0:4:3, :]
+            valid = acc.rearrange("p (q d) -> p q d", q=4)[:, 0:4:3, :]
             if ch == 0:
                 nc.vector.tensor_tensor(out=part[:, h0:h0 + 2, :], in0=valid, in1=w_sb[:, h0:h0 + 2, :], op=ALU.add)
             else:
                 nc.vector.tensor_tensor(out=res[:, h0:h0 + 2, :], in0=valid, in1=part[:, h0:h0 + 2, :], op=ALU.add)
                 nc.sync.dma_start(out=out[b, 2 * pq:2 * pq + 2].rearrange("h s d -> s h d"), in_=res[:, h0:h0 + 2, :])
 
-        load_x(0, 2, [0])
         wraw = const.tile([P, 4, 512], BF16)
-        for w in range(2):
-            nc.sync.dma_start(out=wraw[:, 2 * w:2 * w + 2, :], in_=wv[256 * w:256 * w + 256, :].rearrange("(q e) c -> q e c", e=2))
-        load_x(0, 2, [1])
-        load_x(1, 1, [0])
+        bc = const.tile([P, 512], BF16)
+        w_sb = const.tile([P, 16, DH], BF16)
+        load_x(0)
+        nc.sync.dma_start(out=wraw[:].rearrange("p (hi lo) c -> p hi (lo c)", hi=2), in_=wv.rearrange("(hi p lo) c -> p hi (lo c)", hi=2, lo=2))
+        nc.sync.dma_start(out=bc[:], in_=beta.rearrange("b h (q n) -> (b h q) n", q=NQ))
+        load_x(1)
+        load_vo(0)
+        load_x(2)
+        load_x(3)
+        load_k(0)
+        load_vo(1)
+        load_x(4)
+        load_k(1)
+        load_x(5)
+        load_vo(2)
+        load_k(2)
+        nc.sync.dma_start(out=w_sb[:], in_=W.rearrange("b h s d -> s (b h) d"))
+        load_x(6)
+        load_vo(3)
+        load_k(3)
+        load_x(7)
+        load_vo(4)
+        load_k(4)
         ident_f = const.tile([P, P], F32)
         make_identity(nc, ident_f[:])
         ident_b = const.tile([P, P], BF16)
         make_identity(nc, ident_b[:])
-        bc = const.tile([P, 1024], BF16)
-        nc.vector.memset(bc[64:P, :], 0.0)
-        load_vo(0, [0])
-        load_vo(0, [1])
-        for c in range(NC):
-            nc.sync.dma_start(out=bc[16 * c:16 * c + 16, :].rearrange("p (d0 x) -> p d0 x", x=IL * R), in_=bv[c])
-        load_x(2, 1, [0])
-        load_k(0)
-        load_vo(1, [0, 1])
-        load_x(3, 1, [0])
-        w_sb = const.tile([P, 16, DH], BF16)
-        nc.sync.dma_start(out=w_sb[:], in_=W.rearrange("b h s d -> s (b h) d"))
-        load_k(1)
 
         wgrp = const.tile([P, 512, 4], BF16, align_bytes=64)
         wvw = const.tile([P, 512], U32, align_bytes=64)
@@ -241,97 +210,96 @@ def tile_dpfpattention_pb_t_kernel(tc, x, wv, beta, vo, k_phi, W, out):
             nc.vector.tensor_copy(out=wgrp[:, c0:c1, :], in_=wraw[:, :, c0:c1].rearrange("p t c -> p c t"))
             nc.vector.quantize_mx(out=wvw[:, c0:c1].bitcast(FP8X4), scales=wvs[:, c0:c1], in_=wgrp[:, c0:c1, :].rearrange("p c t -> p (c t)"))
 
+        bank = ps_bank.tile([P, 512], F32, name="bank")
+        acc = bank[:, 256:512]
+        bt = bank[:, 0:256].bitcast(BF16).rearrange("p (j h q) -> p j h q", j=4, q=NQ)
+        beta2 = const.tile([P, STEPS, 8, 4], F32)
+
+        bcv = bc[:].rearrange("p (n j) -> p j n", j=4)
         prep_wv(0, P)
         do_T(0)
-        bt = ps_bt.tile([P, R, P], BF16, name="bt")
-        bcv = bc[:].rearrange("p (q r) -> p q r", r=R)
-        beta2 = const.tile([P, 16, 8, 4], F32)
         for u in range(4):
             do_X(u)
             if u < 3:
                 do_T(u + 1)
             do_QX(u)
-            if u == 3:
-                for r in range(R):
-                    nc.tensor.transpose(bt[:, r, :], bcv[:, :, r], ident_b[:])
             do_S1(0, u)
             if u == 0:
                 prep_wv(P, 2 * P)
                 prep_wv(2 * P, 4 * P)
+                for j in range(4):
+                    nc.tensor.transpose(bt[:, j].rearrange("p h q -> p (h q)"), bcv[:, j, :], ident_b[:])
             if u > 0:
                 do_A(0, u - 1)
-        do_T(4)
-        do_X(4)
-        do_T(5)
-        for b in range(B):
-            for c in range(NC):
-                for rhi in range(2):
-                    if c % 2 == 0 and rhi == 0:
-                        continue
-                    ch, cl = divmod(c, 2)
-                    g0 = 8 * b + 4 * ch
-                    q0 = 2 * (2 * cl + rhi)
-                    row0 = 16 * c + 8 * b
-                    nc.vector.tensor_copy(out=beta2[:, g0:g0 + 4, q0:q0 + 2, :],
-                                          in_=bt[:, 4 * rhi:4 * rhi + 4, row0:row0 + 8].rearrange("p j (pq hh) -> p pq hh j", hh=2))
-        load_x(4, 1, [0])
-        load_vo(2, [0, 1])
-        load_k(2)
+            if u == 1:
+                for b in range(B):
+                    for ch in range(2):
+                        for hh in range(2):
+                            src = bt[:, :, 8 * b + hh:8 * b + 8:2, 4 * ch:4 * ch + 4].rearrange("p j pq ps -> p pq ps j")
+                            g0 = 8 * b + 4 * ch
+                            nc.vector.tensor_copy(out=beta2[:, g0:g0 + 4, hh:8:2, :], in_=src)
+        do_A(0, 3)
 
-        for g in range(0, 17):
-            if g == 0:
-                do_X(5)
-            if 6 <= g + 4 < 16:
-                do_X(g + 4)
-            if g < 16:
+        late_x = {0: [4], 1: [5], 2: [6]}
+        late_x.update({g: [g + 5] for g in range(3, 11)})
+        quant_x = {1: [4], 2: [5], 3: [6, 7]}
+        quant_x.update({g: [g + 4] for g in range(4, 12)})
+
+        for g in range(STEPS):
+            if g > 0:
                 for ps in range(4):
-                    if g > 0 or ps == 3:
-                        do_A(g, ps)
-            if 2 <= g < 16:
+                    do_A(g, ps)
+            if g >= 2:
                 do_FIN(g - 2)
-            if g == 16:
-                do_FIN(15)
-            if g < 16:
-                if g == 0:
-                    new_dv(0)
-                do_Bv(g, 0, 2)
-                if g >= 1:
-                    do_Bv(g - 1, 2, 1)
-                do_KT(g)
-                do_R(g)
-            if 4 <= g + 4 < 16:
-                do_QX(g + 4)
-            if g + 1 < 16:
-                for ps in range(4):
+            if g == 0:
+                new_dv(0)
+            do_Bv(g, 0, 2)
+            if g >= 1:
+                do_Bv(g - 1, 2, 1)
+            if g == 3:
+                do_R(g, [0])
+                do_X(7)
+                do_R(g, [1, 2, 3])
+            else:
+                do_R(g, range(4))
+            for u in quant_x.get(g, []):
+                do_QX(u)
+            if g + 1 < STEPS:
+                for ps in range(3):
                     do_S1(g + 1, ps)
-            if 6 <= g + 5 < 16:
-                do_T(g + 5)
-            if 1 <= g < 16:
+            for u in late_x.get(g, []):
+                do_T(u)
+                do_X(u)
+            if g + 1 < STEPS:
+                do_S1(g + 1, 3)
+            if g >= 1:
                 do_QK(g - 1)
             if g == 0:
                 do_QD(0, 0, 2)
-            if 1 <= g < 16:
+            else:
                 do_QD(g, 0, 8)
                 do_S2(g - 1)
-            if g < 16:
-                new_dv(g + 1)
-            if g < 15:
+            if g == 2:
+                do_T(7)
+            if g + 1 < STEPS:
+                do_KT(g + 1)
+            new_dv(g + 1)
+            if g + 1 < STEPS:
                 do_Bg(g, 3, 5)
-            if g == 15:
-                do_Bv(g, 2, 2)
-                do_Bv(g, 4, 2)
-                do_Bv(g, 6, 2)
-                do_QK(g)
-                do_FIN(g - 1)
-                do_QD(g + 1, 2, 2)
-                do_QD(g + 1, 4, 4)
-                do_S2(g)
-            for i in range(5, 8):
-                if 2 * i - 9 == g:
-                    load_x(i, 1, [0])
-            for k in range(3, 8):
-                if 2 * k - 5 == g:
-                    load_vo(k, [0, 1])
-            for k in range(3, 8):
-                if 2 * k - 5 == g:
-                    load_k(k)
+            if g + 5 < STEPS:
+                if g + 8 < STEPS:
+                    load_x(g + 8)
+                load_vo(g + 5)
+                load_k(g + 5)
+            elif g + 8 < STEPS:
+                load_x(g + 8)
+        g = STEPS - 1
+        do_Bv(g, 2, 2)
+        do_Bv(g, 4, 2)
+        do_Bv(g, 6, 2)
+        do_QK(g)
+        do_FIN(g - 1)
+        do_QD(g + 1, 2, 2)
+        do_QD(g + 1, 4, 4)
+        do_S2(g)
+        do_FIN(g)

@@ -122,10 +122,10 @@ def tile_dpfpattention_pb_t_kernel(tc, x, wv, beta, vo, k_phi, W, out):
 
         def do_A(g, ps):
             if ps == 0:
-                ts[g] = t_pool.tile([P, 8, DH, 4], F32, name="t")
+                ts[g] = t_pool.tile([P, 8, 4, DH], F32, name="t")
             nc.vector.tensor_tensor(out=ts[g][:, 2 * ps:2 * ps + 2],
-                                    in0=s1s[(g, ps)][:].rearrange("p j (hh d) -> p hh d j", hh=2),
-                                    in1=voraws[g][:, :, ps].rearrange("p hh j d -> p hh d j"),
+                                    in0=s1s[(g, ps)][:].rearrange("p j (hh d) -> p hh j d", hh=2),
+                                    in1=voraws[g][:, :, ps],
                                     op=ALU.subtract)
 
         def new_dv(g):
@@ -137,11 +137,11 @@ def tile_dpfpattention_pb_t_kernel(tc, x, wv, beta, vo, k_phi, W, out):
             h0 = 8 * b + 2 * pq + hh0
             bb = bt[:, :, h0:h0 + n, 4 * ch + ps].rearrange("p j hh -> p hh j").unsqueeze(2).to_broadcast([P, n, DH, 4])
             dst = dvgs[g if ps == 0 else g + 1]
-            nc.vector.tensor_tensor(out=dst[:, u0:u0 + n], in0=ts[g][:, u0:u0 + n], in1=bb, op=ALU.mult)
+            nc.vector.tensor_tensor(out=dst[:, u0:u0 + n], in0=ts[g][:, u0:u0 + n].rearrange("p u j d -> p u d j"), in1=bb, op=ALU.mult)
 
         def do_Bg(g, u0, n):
             bb = beta2[:, g, u0:u0 + n, :].unsqueeze(2).to_broadcast([P, n, DH, 4])
-            nc.gpsimd.tensor_tensor(out=dvgs[g + 1][:, u0:u0 + n], in0=ts[g][:, u0:u0 + n], in1=bb, op=ALU.mult)
+            nc.gpsimd.tensor_tensor(out=dvgs[g + 1][:, u0:u0 + n], in0=ts[g][:, u0:u0 + n].rearrange("p u j d -> p u d j"), in1=bb, op=ALU.mult)
 
         def do_QD(g, u0, n):
             if g not in dvws:

@@ -89,8 +89,8 @@ def tile_dpfpattention_pb_t_kernel(tc, x, wv, beta, vo, k_phi, W, out):
         def do_KT(g):
             kts[g] = ps_xt.tile([P, 2, 4 * S], BF16, name="kt", tag="xt")
             for e in range(2):
-                nc.tensor.matmul(out=kts[g][:, e, :].rearrange("p (s j) -> p j s", j=4), lhsT=ident_b[:],
-                                 rhs=kraws[g][:, e, 3], start=True, stop=True)
+                nc.tensor.matmul(out=kts[g][:, e, :].rearrange("p (s jp jl) -> p jp s jl", jp=2, jl=2), lhsT=ident_b[:],
+                                 rhs=kraws[g][:, e, 3].rearrange("p (jp jl) s -> p jp s jl", jp=2), start=True, stop=True)
 
         def do_R(g, pss):
             if g not in kgs:
@@ -129,7 +129,7 @@ def tile_dpfpattention_pb_t_kernel(tc, x, wv, beta, vo, k_phi, W, out):
                                     op=ALU.subtract)
 
         def new_dv(g):
-            dvgs[g] = dv_pool.tile([P, 8, DH, 4], BF16, name="dvg", tag="last" if g == STEPS else "dvg", align_bytes=64)
+            dvgs[g] = dv_pool.tile([P, 8, DH, 4], BF16, name="dvg", tag="edge" if g % STEPS == 0 else "dvg", align_bytes=64)
 
         def do_Bv(g, u0, n):
             b, ch, pq = where(g)
@@ -232,9 +232,9 @@ def tile_dpfpattention_pb_t_kernel(tc, x, wv, beta, vo, k_phi, W, out):
             if u > 0:
                 do_A(0, u - 1)
             if u == 1:
-                for b in range(B):
-                    for ch in range(2):
-                        for hh in range(2):
+                for hh in range(2):
+                    for b in range(B):
+                        for ch in range(2):
                             src = bt[:, :, 8 * b + hh:8 * b + 8:2, 4 * ch:4 * ch + 4].rearrange("p j pq ps -> p pq ps j")
                             g0 = 8 * b + 4 * ch
                             nc.vector.tensor_copy(out=beta2[:, g0:g0 + 4, hh:8:2, :], in_=src)
@@ -256,6 +256,11 @@ def tile_dpfpattention_pb_t_kernel(tc, x, wv, beta, vo, k_phi, W, out):
             do_Bv(g, 0, 2)
             if g >= 1:
                 do_Bv(g - 1, 2, 1)
+            if g == STEPS - 1:
+                new_dv(g + 1)
+                do_Bv(g, 2, 2)
+                do_Bv(g, 4, 2)
+                do_Bg(g, 6, 2)
             if g == 3:
                 do_R(g, [0])
                 do_X(7)
@@ -272,19 +277,19 @@ def tile_dpfpattention_pb_t_kernel(tc, x, wv, beta, vo, k_phi, W, out):
                 do_X(u)
             if g + 1 < STEPS:
                 do_S1(g + 1, 3)
+            if g == 1:
+                do_QD(0, 0, 2)
             if g >= 1:
                 do_QK(g - 1)
-            if g == 0:
-                do_QD(0, 0, 2)
-            else:
+            if g >= 1:
                 do_QD(g, 0, 8)
                 do_S2(g - 1)
             if g == 2:
                 do_T(7)
             if g + 1 < STEPS:
                 do_KT(g + 1)
-            new_dv(g + 1)
             if g + 1 < STEPS:
+                new_dv(g + 1)
                 do_Bg(g, 3, 5)
             if g + 5 < STEPS:
                 if g + 8 < STEPS:
@@ -294,9 +299,6 @@ def tile_dpfpattention_pb_t_kernel(tc, x, wv, beta, vo, k_phi, W, out):
             elif g + 8 < STEPS:
                 load_x(g + 8)
         g = STEPS - 1
-        do_Bv(g, 2, 2)
-        do_Bv(g, 4, 2)
-        do_Bv(g, 6, 2)
         do_QK(g)
         do_FIN(g - 1)
         do_QD(g + 1, 2, 2)

@@ -15,6 +15,7 @@ P = 128
 FLOPS = 2 * B * N * D * (H * DH) + 2 * B * H * N * S * DH
 
 NQ = 8
+S0 = 64
 STEPS = 16
 
 
@@ -87,21 +88,27 @@ def tile_dpfpattention_pb_t_kernel(tc, x, wv, beta, vo, k_phi, W, out):
             xws[u] = (xw, xs)
 
         def do_KT(g):
-            kts[g] = ps_xt.tile([P, 2, 4 * S], BF16, name="kt", tag="xt")
-            for e in range(2):
-                nc.tensor.matmul(out=kts[g][:, e, :].rearrange("p (s jp jl) -> p jp s jl", jp=2, jl=2), lhsT=ident_b[:],
-                                 rhs=kraws[g][:, e, 3].rearrange("p (jp jl) s -> p jp s jl", jp=2), start=True, stop=True)
+            kts[g] = ps_xt.tile([P, 2 * S - S0, 4], BF16, name="kt", tag="xt")
+            kt = kts[g][:].rearrange("p s (jp jl) -> p jp s jl", jp=2)
+            k0 = kraws[g][:, 0, 3, :, S0:S].rearrange("p (jp jl) s -> p jp s jl", jp=2)
+            k1 = kraws[g][:, 1, 0].rearrange("p (jp jl) s -> p jp s jl", jp=2)
+            nc.tensor.matmul(out=kt[:, :, 0:S - S0, :], lhsT=ident_b[:], rhs=k0, start=True, stop=True)
+            nc.tensor.matmul(out=kt[:, :, S - S0:2 * S - S0, :], lhsT=ident_b[:], rhs=k1, start=True, stop=True)
 
-        def do_R(g, pss):
-            if g not in kgs:
+        def do_R(g, part):
+            if part == 0:
                 kgs[g] = kg_pool.tile([P, 2, 4, S, 4], BF16, name="kg", align_bytes=64)
-            for ps in pss:
-                if ps == 3 and g in kts:
-                    nc.scalar.copy(out=kgs[g][:, :, 3].rearrange("p e s j -> p e (s j)"), in_=kts[g][:])
-                    continue
-                for e in range(2):
-                    nc.scalar.copy(out=kgs[g][:, e, ps].rearrange("p (c i) j -> p c j i", i=4),
-                                   in_=kraws[g][:, e, ps].rearrange("p j (c i) -> p c j i", i=4))
+                todo = [(0, 0, S), (1, 1, S)]
+            else:
+                todo = [(0, 1, S), (1, 2, S), (0, 2, S), (1, 3, S), (0, 3, S0 if g in kts else S)]
+                if g not in kts:
+                    todo.append((1, 0, S))
+            for e, ps, s1 in todo:
+                nc.scalar.copy(out=kgs[g][:, e, ps, 0:s1].rearrange("p (c i) j -> p c j i", i=4),
+                               in_=kraws[g][:, e, ps, :, 0:s1].rearrange("p j (c i) -> p c j i", i=4))
+            if part == 1 and g in kts:
+                flat = kgs[g][:].rearrange("p e q s j -> p (e q s) j")
+                nc.scalar.copy(out=flat[:, 3 * S + S0:5 * S, :], in_=kts[g][:])
 
         def do_QK(g):
             kw = kw_pool.tile([P, 1024], U32, name="kw", align_bytes=64)
@@ -178,10 +185,10 @@ def tile_dpfpattention_pb_t_kernel(tc, x, wv, beta, vo, k_phi, W, out):
         w_sb = const.tile([P, 16, DH], BF16)
         load_x(0)
         nc.sync.dma_start(out=wraw[:].rearrange("p (hi lo) c -> p hi (lo c)", hi=2), in_=wv.rearrange("(hi p lo) c -> p hi (lo c)", hi=2, lo=2))
-        nc.sync.dma_start(out=bc[:], in_=beta.rearrange("b h (q n) -> (b h q) n", q=NQ))
         load_x(1)
-        load_vo(0)
+        nc.sync.dma_start(out=bc[:], in_=beta.rearrange("b h (q n) -> (b h q) n", q=NQ))
         load_x(2)
+        load_vo(0)
         load_x(3)
         load_k(0)
         load_vo(1)
@@ -242,7 +249,7 @@ def tile_dpfpattention_pb_t_kernel(tc, x, wv, beta, vo, k_phi, W, out):
 
         late_x = {0: [4], 1: [5], 2: [6]}
         late_x.update({g: [g + 5] for g in range(3, 11)})
-        quant_x = {1: [4], 2: [5], 3: [6, 7]}
+        quant_x = {1: [4], 2: [5], 3: [6]}
         quant_x.update({g: [g + 4] for g in range(4, 12)})
 
         for g in range(STEPS):
@@ -261,12 +268,10 @@ def tile_dpfpattention_pb_t_kernel(tc, x, wv, beta, vo, k_phi, W, out):
                 do_Bv(g, 2, 2)
                 do_Bv(g, 4, 2)
                 do_Bg(g, 6, 2)
+            do_R(g, 0)
             if g == 3:
-                do_R(g, [0])
                 do_X(7)
-                do_R(g, [1, 2, 3])
-            else:
-                do_R(g, range(4))
+            do_R(g, 1)
             for u in quant_x.get(g, []):
                 do_QX(u)
             if g + 1 < STEPS:
@@ -275,12 +280,14 @@ def tile_dpfpattention_pb_t_kernel(tc, x, wv, beta, vo, k_phi, W, out):
             for u in late_x.get(g, []):
                 do_T(u)
                 do_X(u)
-            if g + 1 < STEPS:
-                do_S1(g + 1, 3)
             if g == 1:
                 do_QD(0, 0, 2)
             if g >= 1:
                 do_QK(g - 1)
+            if g == 3:
+                do_QX(7)
+            if g + 1 < STEPS:
+                do_S1(g + 1, 3)
             if g >= 1:
                 do_QD(g, 0, 8)
                 do_S2(g - 1)

@@ -23,7 +23,7 @@ def tile_dpfpattention_pb_t_kernel(tc, x, wv, beta, vo, k_phi, W, out):
     nc = tc.nc
     with ExitStack() as ctx:
         const = ctx.enter_context(tc.tile_pool(name="const", bufs=1))
-        x_pool = ctx.enter_context(tc.tile_pool(name="x", bufs=8))
+        x_pool = ctx.enter_context(tc.tile_pool(name="x", bufs=9))
         xg_pool = ctx.enter_context(tc.tile_pool(name="xg", bufs=3))
         vo_pool = ctx.enter_context(tc.tile_pool(name="vo", bufs=6))
         k_pool = ctx.enter_context(tc.tile_pool(name="k", bufs=6))
@@ -129,26 +129,27 @@ def tile_dpfpattention_pb_t_kernel(tc, x, wv, beta, vo, k_phi, W, out):
 
         def do_A(g, ps):
             if ps == 0:
-                ts[g] = t_pool.tile([P, 8, 4, DH], F32, name="t")
+                ts[g] = t_pool.tile([P, 8, DH, 4], F32, name="t")
             nc.vector.tensor_tensor(out=ts[g][:, 2 * ps:2 * ps + 2],
-                                    in0=s1s[(g, ps)][:].rearrange("p j (hh d) -> p hh j d", hh=2),
-                                    in1=voraws[g][:, :, ps],
+                                    in0=s1s[(g, ps)][:].rearrange("p j (hh d) -> p hh d j", hh=2),
+                                    in1=voraws[g][:, :, ps].rearrange("p hh j d -> p hh d j"),
                                     op=ALU.subtract)
 
         def new_dv(g):
             dvgs[g] = dv_pool.tile([P, 8, DH, 4], BF16, name="dvg", tag="edge" if g % STEPS == 0 else "dvg", align_bytes=64)
 
-        def do_Bv(g, u0, n):
-            b, ch, pq = where(g)
-            ps, hh0 = divmod(u0, 2)
-            h0 = 8 * b + 2 * pq + hh0
-            bb = bt[:, :, h0:h0 + n, 4 * ch + ps].rearrange("p j hh -> p hh j").unsqueeze(2).to_broadcast([P, n, DH, 4])
-            dst = dvgs[g if ps == 0 else g + 1]
-            nc.vector.tensor_tensor(out=dst[:, u0:u0 + n], in0=ts[g][:, u0:u0 + n].rearrange("p u j d -> p u d j"), in1=bb, op=ALU.mult)
+        def halves(tile, a, b):
+            return tile[:].rearrange("p u (f d) j -> p (u f) d j", f=2)[:, a:b]
 
-        def do_Bg(g, u0, n):
-            bb = beta2[:, g, u0:u0 + n, :].unsqueeze(2).to_broadcast([P, n, DH, 4])
-            nc.gpsimd.tensor_tensor(out=dvgs[g + 1][:, u0:u0 + n], in0=ts[g][:, u0:u0 + n].rearrange("p u j d -> p u d j"), in1=bb, op=ALU.mult)
+        def do_Bv(g, a, b):
+            for u0, u1, d0, d1 in [(a // 2, b // 2, 0, DH)] if a % 2 == 0 and b % 2 == 0 else [(a // 2, a // 2 + 1, 32 * (a % 2), 32 * (a % 2) + 32 * (b - a))]:
+                bb = bt[:, :, 8 * g + u0:8 * g + u1].rearrange("p j u -> p u j").unsqueeze(2).to_broadcast([P, u1 - u0, d1 - d0, 4])
+                dst = dvgs[g if u1 <= 2 else g + 1]
+                nc.vector.tensor_tensor(out=dst[:, u0:u1, d0:d1], in0=ts[g][:, u0:u1, d0:d1], in1=bb, op=ALU.mult)
+
+        def do_Bg(g, a, b):
+            bb = beta2[:, g, a:b, :].unsqueeze(2).to_broadcast([P, b - a, DH // 2, 4])
+            nc.gpsimd.tensor_tensor(out=halves(dvgs[g + 1], a, b), in0=halves(ts[g], a, b), in1=bb, op=ALU.mult)
 
         def do_QD(g, u0, n):
             if g not in dvws:
@@ -202,12 +203,18 @@ def tile_dpfpattention_pb_t_kernel(tc, x, wv, beta, vo, k_phi, W, out):
         load_vo(3)
         load_k(3)
         load_x(7)
+        load_x(8)
         load_vo(4)
         load_k(4)
         ident_f = const.tile([P, P], F32)
         make_identity(nc, ident_f[:])
         ident_b = const.tile([P, P], BF16)
         make_identity(nc, ident_b[:])
+        perm = const.tile([P, P], BF16)
+        for bch in range(4):
+            b, ch = divmod(bch, 2)
+            rows = ident_b[:, 64 * b:64 * b + 64].rearrange("p (pq hh c q) -> p c pq q hh", pq=4, hh=2, c=2)
+            nc.vector.tensor_copy(out=perm[:, 32 * bch:32 * bch + 32].rearrange("p (pq q hh) -> p pq q hh", pq=4, q=4), in_=rows[:, ch])
 
         wgrp = const.tile([P, 512, 4], BF16, align_bytes=64)
         wvw = const.tile([P, 512], U32, align_bytes=64)
@@ -219,8 +226,8 @@ def tile_dpfpattention_pb_t_kernel(tc, x, wv, beta, vo, k_phi, W, out):
 
         bank = ps_bank.tile([P, 512], F32, name="bank")
         acc = bank[:, 256:512]
-        bt = bank[:, 0:256].bitcast(BF16).rearrange("p (j h q) -> p j h q", j=4, q=NQ)
-        beta2 = const.tile([P, STEPS, 8, 4], F32)
+        bt = bank[:, 0:256].bitcast(BF16).rearrange("p (j r) -> p j r", j=4)
+        beta2 = const.tile([P, STEPS, 16, 4], F32)
 
         bcv = bc[:].rearrange("p (n j) -> p j n", j=4)
         prep_wv(0, P)
@@ -235,16 +242,12 @@ def tile_dpfpattention_pb_t_kernel(tc, x, wv, beta, vo, k_phi, W, out):
                 prep_wv(P, 2 * P)
                 prep_wv(2 * P, 4 * P)
                 for j in range(4):
-                    nc.tensor.transpose(bt[:, j].rearrange("p h q -> p (h q)"), bcv[:, j, :], ident_b[:])
+                    nc.tensor.transpose(bt[:, j], bcv[:, j, :], perm[:])
             if u > 0:
                 do_A(0, u - 1)
             if u == 1:
-                for hh in range(2):
-                    for b in range(B):
-                        for ch in range(2):
-                            src = bt[:, :, 8 * b + hh:8 * b + 8:2, 4 * ch:4 * ch + 4].rearrange("p j pq ps -> p pq ps j")
-                            g0 = 8 * b + 4 * ch
-                            nc.vector.tensor_copy(out=beta2[:, g0:g0 + 4, hh:8:2, :], in_=src)
+                src = bt.rearrange("p j r -> p r j").unsqueeze(2).to_broadcast([P, P, 2, 4])
+                nc.scalar.copy(out=beta2[:].rearrange("p g (u f) j -> p (g u) f j", f=2), in_=src)
         do_A(0, 3)
 
         late_x = {0: [4], 1: [5], 2: [6]}
@@ -260,14 +263,13 @@ def tile_dpfpattention_pb_t_kernel(tc, x, wv, beta, vo, k_phi, W, out):
                 do_FIN(g - 2)
             if g == 0:
                 new_dv(0)
-            do_Bv(g, 0, 2)
+            do_Bv(g, 0, 4)
             if g >= 1:
-                do_Bv(g - 1, 2, 1)
+                do_Bv(g - 1, 4, 5)
             if g == STEPS - 1:
                 new_dv(g + 1)
-                do_Bv(g, 2, 2)
-                do_Bv(g, 4, 2)
-                do_Bg(g, 6, 2)
+                do_Bv(g, 4, 12)
+                do_Bg(g, 12, 16)
             do_R(g, 0)
             if g == 3:
                 do_X(7)
@@ -277,7 +279,7 @@ def tile_dpfpattention_pb_t_kernel(tc, x, wv, beta, vo, k_phi, W, out):
             if g + 1 < STEPS:
                 for ps in range(3):
                     do_S1(g + 1, ps)
-            for u in late_x.get(g, []):
+            for u in late_x.get(g, []) if g != 3 else []:
                 do_T(u)
                 do_X(u)
             if g == 1:
@@ -288,6 +290,9 @@ def tile_dpfpattention_pb_t_kernel(tc, x, wv, beta, vo, k_phi, W, out):
                 do_QX(7)
             if g + 1 < STEPS:
                 do_S1(g + 1, 3)
+            if g == 3:
+                do_T(g + 5)
+                do_X(g + 5)
             if g >= 1:
                 do_QD(g, 0, 8)
                 do_S2(g - 1)
@@ -297,14 +302,14 @@ def tile_dpfpattention_pb_t_kernel(tc, x, wv, beta, vo, k_phi, W, out):
                 do_KT(g + 1)
             if g + 1 < STEPS:
                 new_dv(g + 1)
-                do_Bg(g, 3, 5)
+                do_Bg(g, 5, 16)
             if g + 5 < STEPS:
-                if g + 8 < STEPS:
-                    load_x(g + 8)
+                if g + 9 < STEPS:
+                    load_x(g + 9)
                 load_vo(g + 5)
                 load_k(g + 5)
-            elif g + 8 < STEPS:
-                load_x(g + 8)
+            elif g + 9 < STEPS:
+                load_x(g + 9)
         g = STEPS - 1
         do_QK(g)
         do_FIN(g - 1)

from contextlib import ExitStack

import concourse.mybir as mybir
from concourse.masks import make_identity

FP8X4 = mybir.dt.float8_e4m3fn_x4
BF16 = mybir.dt.bfloat16
F32 = mybir.dt.float32
U32 = mybir.dt.uint32
U8 = mybir.dt.uint8
ALU = mybir.AluOpType

B, N, D, H, DH, S = 2, 4096, 512, 8, 64, 128
P = 128
FLOPS = 2 * B * N * D * (H * DH) + 2 * B * H * N * S * DH

NQ = 8
S0 = 64
STEPS = 16


def tile_dpfpattention_pb_t_kernel(tc, x, wv, beta, vo, k_phi, W, out):
    nc = tc.nc
    with ExitStack() as ctx:
        const = ctx.enter_context(tc.tile_pool(name="const", bufs=1))
        x_pool = ctx.enter_context(tc.tile_pool(name="x", bufs=9))
        xg_pool = ctx.enter_context(tc.tile_pool(name="xg", bufs=3))
        vo_pool = ctx.enter_context(tc.tile_pool(name="vo", bufs=6))
        k_pool = ctx.enter_context(tc.tile_pool(name="k", bufs=6))
        xw_pool = ctx.enter_context(tc.tile_pool(name="xw", bufs=8))
        kg_pool = ctx.enter_context(tc.tile_pool(name="kg", bufs=2))
        kw_pool = ctx.enter_context(tc.tile_pool(name="kw", bufs=2))
        t_pool = ctx.enter_context(tc.tile_pool(name="t", bufs=3))
        dv_pool = ctx.enter_context(tc.tile_pool(name="dv", bufs=1))
        ps_bank = ctx.enter_context(tc.psum_pool(name="ps_bank", bufs=1))
        ps_s1 = ctx.enter_context(tc.psum_pool(name="ps_s1", bufs=4))
        ps_xt = ctx.enter_context(tc.psum_pool(name="ps_xt", bufs=3))
        ctx.enter_context(tc.manual_schedule())

        xv = x.rearrange("b (q p j) k -> b q p j k", p=P, j=4)
        vv = vo.rearrange("b h (q p j) d -> b h p q (j d)", p=P, j=4)
        kv = k_phi.rearrange("b h (q p j) s -> b h p q (j s)", p=P, j=4)

        part = const.tile([P, 16, DH], F32)
        res = const.tile([P, 16, DH], F32)
        xraws, voraws, kraws, xws = {}, {}, {}, {}
        xts, xgs, kts, kgs, kws, s1s, ts, dvgs, dvws = {}, {}, {}, {}, {}, {}, {}, {}, {}

        def where(g):
            return g // 8, (g // 4) % 2, g % 4

        def load_x(u):
            xraws[u] = x_pool.tile([P, 4, D], BF16, name="xraw")
            nc.sync.dma_start(out=xraws[u][:], in_=xv[u // NQ, u % NQ])

        def load_vo(g):
            b, ch, pq = where(g)
            voraws[g] = vo_pool.tile([P, 2, 4, 4, DH], BF16, name="voraw")
            for e in range(2):
                nc.sync.dma_start(out=voraws[g][:, e].rearrange("p q j d -> p q (j d)"), in_=vv[b, 2 * pq + e][:, 4 * ch:4 * ch + 4, :])

        def load_k(g):
            b, ch, pq = where(g)
            kraws[g] = k_pool.tile([P, 2, 4, 4, S], BF16, name="kraw")
            for e in range(2):
                nc.sync.dma_start(out=kraws[g][:, e].rearrange("p q j s -> p q (j s)"), in_=kv[b, 2 * pq + e][:, 4 * ch:4 * ch + 4, :])

        def do_T(u):
            x32 = xraws[u][:].bitcast(F32)
            xts[u] = []
            for jp in range(2):
                xt = ps_xt.tile([P, 2, 2, P], F32, name="xt", tag="xt")
                for jl in range(2):
                    for w in range(2):
                        nc.tensor.transpose(xt[:, jl, w, :], x32[:, 2 * jp + jl, P * w:P * w + P], ident_f[:])
                xts[u].append(xt)

        def do_X(u):
            xgs[u] = xg_pool.tile([P, 4, P, 4], BF16, name="xg", align_bytes=64)
            xg32 = xgs[u][:].bitcast(F32)
            for jp in range(2):
                nc.scalar.copy(out=xg32[:, 2 * jp:2 * jp + 2, :, :], in_=xts[u][jp][:].rearrange("p jl w m -> p jl m w"))

        def do_QX(u):
            xw = xw_pool.tile([P, 512], U32, name="xw", align_bytes=64)
            xs = xw_pool.tile([P, 512], U8, name="xs", align_bytes=64)
            nc.vector.quantize_mx(out=xw[:].bitcast(FP8X4), scales=xs[:], in_=xgs[u][:].rearrange("p j m t -> p (j m t)"))
            xws[u] = (xw, xs)

        def do_KT(g):
            kts[g] = ps_xt.tile([P, 2 * S - S0, 4], BF16, name="kt", tag="xt")
            kt = kts[g][:].rearrange("p s (jp jl) -> p jp s jl", jp=2)
            k0 = kraws[g][:, 0, 3, :, S0:S].rearrange("p (jp jl) s -> p jp s jl", jp=2)
            k1 = kraws[g][:, 1, 0].rearrange("p (jp jl) s -> p jp s jl", jp=2)
            nc.tensor.matmul(out=kt[:, :, 0:S - S0, :], lhsT=ident_b[:], rhs=k0, start=True, stop=True)
            nc.tensor.matmul(out=kt[:, :, S - S0:2 * S - S0, :], lhsT=ident_b[:], rhs=k1, start=True, stop=True)

        def do_R(g, part):
            if part == 0:
                kgs[g] = kg_pool.tile([P, 2, 4, S, 4], BF16, name="kg", align_bytes=64)
                todo = [(0, 0, S), (1, 1, S)]
            else:
                todo = [(0, 1, S), (1, 2, S), (0, 2, S), (1, 3, S), (0, 3, S0 if g in kts else S)]
                if g not in kts:
                    todo.append((1, 0, S))
            for e, ps, s1 in todo:
                nc.scalar.copy(out=kgs[g][:, e, ps, 0:s1].rearrange("p (c i) j -> p c j i", i=4),
                               in_=kraws[g][:, e, ps, :, 0:s1].rearrange("p j (c i) -> p c j i", i=4))
            if part == 1 and g in kts:
                flat = kgs[g][:].rearrange("p e q s j -> p (e q s) j")
                nc.scalar.copy(out=flat[:, 3 * S + S0:5 * S, :], in_=kts[g][:])

        def do_QK(g):
            kw = kw_pool.tile([P, 1024], U32, name="kw", align_bytes=64)
            ks = kw_pool.tile([P, 1024], U8, name="ks", align_bytes=64)
            nc.vector.quantize_mx(out=kw[:].bitcast(FP8X4), scales=ks[:], in_=kgs[g][:].rearrange("p e q s j -> p (e q s j)"))
            kws[g] = (kw, ks)

        def do_S1(g, ps):
            pq = g % 4
            xw, xs = xws[4 * (g // 4) + ps]
            s1 = ps_s1.tile([P, 4, P], F32, name="s1", tag="s1")
            for j in range(4):
                nc.tensor.matmul_mx(out=s1[:, j, :],
                                    lhsT=xw[:, P * j:P * j + P].bitcast(FP8X4), lhsT_scale=xs[:, P * j:P * j + P],
                                    rhs=wvw[:, P * pq:P * pq + P].bitcast(FP8X4), rhs_scale=wvs[:, P * pq:P * pq + P],
                                    start=True, stop=True)
            s1s[(g, ps)] = s1

        def do_A(g, ps):
            if ps == 0:
                ts[g] = t_pool.tile([P, 8, DH, 4], F32, name="t")
            nc.vector.tensor_tensor(out=ts[g][:, 2 * ps:2 * ps + 2],
                                    in0=s1s[(g, ps)][:].rearrange("p j (hh d) -> p hh d j", hh=2),
                                    in1=voraws[g][:, :, ps].rearrange("p hh j d -> p hh d j"),
                                    op=ALU.subtract)

        def new_dv(g):
            dvgs[g] = dv_pool.tile([P, 8, DH, 4], BF16, name="dvg", tag="edge" if g % STEPS == 0 else "dvg", align_bytes=64)

        def halves(tile, a, b):
            return tile[:].rearrange("p u (f d) j -> p (u f) d j", f=2)[:, a:b]

        def do_Bv(g, a, b):
            for u0, u1, d0, d1 in [(a // 2, b // 2, 0, DH)] if a % 2 == 0 and b % 2 == 0 else [(a // 2, a // 2 + 1, 32 * (a % 2), 32 * (a % 2) + 32 * (b - a))]:
                bb = bt[:, :, 8 * g + u0:8 * g + u1].rearrange("p j u -> p u j").unsqueeze(2).to_broadcast([P, u1 - u0, d1 - d0, 4])
                dst = dvgs[g if u1 <= 2 else g + 1]
                nc.vector.tensor_tensor(out=dst[:, u0:u1, d0:d1], in0=ts[g][:, u0:u1, d0:d1], in1=bb, op=ALU.mult)

        def do_Bg(g, a, b):
            bb = beta2[:, g, a:b, :].unsqueeze(2).to_broadcast([P, b - a, DH // 2, 4])
            nc.gpsimd.tensor_tensor(out=halves(dvgs[g + 1], a, b), in0=halves(ts[g], a, b), in1=bb, op=ALU.mult)

        def do_QD(g, u0, n):
            if g not in dvws:
                dvw = dv_pool.tile([P, 8 * DH], U32, name="dvw", align_bytes=64, bufs=3)
                dvs = dv_pool.tile([P, 8 * DH], U8, name="dvs", align_bytes=64, bufs=3)
                dvws[g] = (dvw, dvs)
            dvw, dvs = dvws[g]
            nc.vector.quantize_mx(out=dvw[:, DH * u0:DH * (u0 + n)].bitcast(FP8X4), scales=dvs[:, DH * u0:DH * (u0 + n)],
                                  in_=dvgs[g][:, u0:u0 + n].rearrange("p q d j -> p (q d j)"))

        def do_S2(g):
            kw, ks = kws[g]
            for e in range(2):
                for ps in range(4):
                    dvw, dvs = dvws[g if ps == 0 else g + 1]
                    o = (4 * e + ps) * P
                    nc.tensor.matmul_mx(out=acc[:, P * e:P * e + P],
                                        lhsT=kw[:, o:o + P].bitcast(FP8X4), lhsT_scale=ks[:, o:o + P],
                                        rhs=dvw[:, P * ps:P * ps + P].bitcast(FP8X4), rhs_scale=dvs[:, P * ps:P * ps + P],
                                        start=(ps == 0), stop=(ps == 3))

        def do_FIN(g):
            b, ch, pq = where(g)
            h0 = 8 * b + 2 * pq
            valid = acc.rearrange("p (q d) -> p q d", q=4)[:, 0:4:3, :]
            if ch == 0:
                nc.vector.tensor_tensor(out=part[:, h0:h0 + 2, :], in0=valid, in1=w_sb[:, h0:h0 + 2, :], op=ALU.add)
            else:
                nc.vector.tensor_tensor(out=res[:, h0:h0 + 2, :], in0=valid, in1=part[:, h0:h0 + 2, :], op=ALU.add)
                nc.sync.dma_start(out=out[b, 2 * pq:2 * pq + 2].rearrange("h s d -> s h d"), in_=res[:, h0:h0 + 2, :])

        wraw = const.tile([P, 4, 512], BF16)
        bc = const.tile([P, 512], BF16)
        w_sb = const.tile([P, 16, DH], BF16)
        load_x(0)
        nc.sync.dma_start(out=wraw[:].rearrange("p (hi lo) c -> p hi (lo c)", hi=2), in_=wv.rearrange("(hi p lo) c -> p hi (lo c)", hi=2, lo=2))
        load_x(1)
        nc.sync.dma_start(out=bc[:], in_=beta.rearrange("b h (q n) -> (b h q) n", q=NQ))
        load_x(2)
        load_vo(0)
        load_x(3)
        load_k(0)
        load_vo(1)
        load_x(4)
        load_k(1)
        load_x(5)
        load_vo(2)
        load_k(2)
        nc.sync.dma_start(out=w_sb[:], in_=W.rearrange("b h s d -> s (b h) d"))
        load_x(6)
        load_vo(3)
        load_k(3)
        load_x(7)
        load_x(8)
        load_vo(4)
        load_k(4)
        ident_f = const.tile([P, P], F32)
        make_identity(nc, ident_f[:])
        ident_b = const.tile([P, P], BF16)
        make_identity(nc, ident_b[:])
        perm = const.tile([P, P], BF16)
        for bch in range(4):
            b, ch = divmod(bch, 2)
            rows = ident_b[:, 64 * b:64 * b + 64].rearrange("p (pq hh c q) -> p c pq q hh", pq=4, hh=2, c=2)
            nc.vector.tensor_copy(out=perm[:, 32 * bch:32 * bch + 32].rearrange("p (pq q hh) -> p pq q hh", pq=4, q=4), in_=rows[:, ch])

        wgrp = const.tile([P, 512, 4], BF16, align_bytes=64)
        wvw = const.tile([P, 512], U32, align_bytes=64)
        wvs = const.tile([P, 512], U8, align_bytes=64)

        def prep_wv(c0, c1):
            nc.vector.tensor_copy(out=wgrp[:, c0:c1, :], in_=wraw[:, :, c0:c1].rearrange("p t c -> p c t"))
            nc.vector.quantize_mx(out=wvw[:, c0:c1].bitcast(FP8X4), scales=wvs[:, c0:c1], in_=wgrp[:, c0:c1, :].rearrange("p c t -> p (c t)"))

        bank = ps_bank.tile([P, 512], F32, name="bank")
        acc = bank[:, 256:512]
        bt = bank[:, 0:256].bitcast(BF16).rearrange("p (j r) -> p j r", j=4)
        beta2 = const.tile([P, STEPS, 16, 4], F32)

        bcv = bc[:].rearrange("p (n j) -> p j n", j=4)
        prep_wv(0, P)
        do_T(0)
        for u in range(4):
            do_X(u)
            if u < 3:
                do_T(u + 1)
            do_QX(u)
            do_S1(0, u)
            if u == 0:
                prep_wv(P, 2 * P)
                prep_wv(2 * P, 4 * P)
                for j in range(4):
                    nc.tensor.transpose(bt[:, j], bcv[:, j, :], perm[:])
            if u > 0:
                do_A(0, u - 1)
            if u == 1:
                src = bt.rearrange("p j r -> p r j").unsqueeze(2).to_broadcast([P, P, 2, 4])
                nc.scalar.copy(out=beta2[:].rearrange("p g (u f) j -> p (g u) f j", f=2), in_=src)
        do_A(0, 3)

        late_x = {0: [4], 1: [5], 2: [6]}
        late_x.update({g: [g + 5] for g in range(3, 11)})
        quant_x = {1: [4], 2: [5], 3: [6]}
        quant_x.update({g: [g + 4] for g in range(4, 12)})

        for g in range(STEPS):
            if g > 0:
                for ps in range(4):
                    do_A(g, ps)
            if g >= 2:
                do_FIN(g - 2)
            if g == 0:
                new_dv(0)
            do_Bv(g, 0, 4)
            if g >= 1:
                do_Bv(g - 1, 4, 5)
            if g == STEPS - 1:
                new_dv(g + 1)
                do_Bv(g, 4, 12)
                do_Bg(g, 12, 16)
            do_R(g, 0)
            if g == 3:
                do_X(7)
            do_R(g, 1)
            for u in quant_x.get(g, []):
                do_QX(u)
            if g + 1 < STEPS:
                for ps in range(3):
                    do_S1(g + 1, ps)
            for u in late_x.get(g, []) if g != 3 else []:
                do_T(u)
                do_X(u)
            if g == 1:
                do_QD(0, 0, 2)
            if g >= 1:
                do_QK(g - 1)
            if g == 3:
                do_QX(7)
            if g + 1 < STEPS:
                do_S1(g + 1, 3)
            if g == 3:
                do_T(g + 5)
                do_X(g + 5)
            if g >= 1:
                do_QD(g, 0, 8)
                do_S2(g - 1)
            if g == 2:
                do_T(7)
            if g + 1 < STEPS:
                do_KT(g + 1)
            if g + 1 < STEPS:
                new_dv(g + 1)
                do_Bg(g, 5, 16)
            if g + 5 < STEPS:
                if g + 9 < STEPS:
                    load_x(g + 9)
                load_vo(g + 5)
                load_k(g + 5)
            elif g + 9 < STEPS:
                load_x(g + 9)
        g = STEPS - 1
        do_QK(g)
        do_FIN(g - 1)
        do_QD(g + 1, 2, 2)
        do_QD(g + 1, 4, 4)
        do_S2(g)
        do_FIN(g)
